import numpy as np
import ml_dtypes


def mxq(x, axis, fmt="e4m3"):
    dtype, down = {"e4m3": (ml_dtypes.float8_e4m3fn, 7), "e5m2": (ml_dtypes.float8_e5m2, 14)}[fmt]
    v = np.moveaxis(np.asarray(x, np.float32).astype(ml_dtypes.bfloat16).astype(np.float64), axis, -1)
    blocks = v.reshape(v.shape[:-1] + (-1, 32))
    amax = np.abs(blocks).max(-1, keepdims=True)
    byte = np.maximum(np.where(amax > 0, np.frexp(amax)[1] - 1 + 127, 0) - down, 1)
    scale = np.exp2(byte - 127.0)
    codes = (blocks / scale).astype(np.float32).astype(dtype).astype(np.float64)
    return np.moveaxis((codes * scale).reshape(v.shape), -1, axis)


WIDE = False


def mx_kscale(k):
    if not WIDE:
        return np.ones(k)
    levels = np.array([10, -10, 5, -5, 0])
    a = np.random.permutation(np.resize(levels, k // 512 * 4)).reshape(k // 512, 4)
    idx = np.arange(k)
    return np.exp2(a[idx // 512, idx % 128 // 32])


BF16 = ml_dtypes.bfloat16


def bf(x):
    return np.asarray(x, np.float32).astype(BF16)


def f64(x):
    return np.asarray(x).astype(np.float64)


E2M1 = np.array([0.0, 0.5, 1.0, 1.5, 2.0, 3.0, 4.0, 6.0, -0.0, -0.5, -1.0, -1.5, -2.0, -3.0, -4.0, -6.0])


def pack_weight(w, fmt):
    k, n = w.shape
    w = f64(bf(w)).reshape(k // 32, 32, n)
    amax = np.abs(w).max(1)
    if fmt == "e4m3":
        byte = np.frexp(amax)[1] - 1 + 127 - 7
    else:
        mant, ex = np.frexp(amax / 6.0)
        byte = np.where(mant > 0.5, ex, ex - 1) + 127
    byte = np.clip(np.where(amax > 0, byte, 1), 1, 254)
    scaled = (w * np.exp2(127.0 - byte)[:, None, :]).reshape(k, n).astype(np.float32)
    by_word = np.ascontiguousarray(scaled.reshape(k // 512, 128, 4, n).transpose(0, 1, 3, 2))
    if fmt == "e4m3":
        words = by_word.astype(ml_dtypes.float8_e4m3fn).view(np.uint8)
    else:
        c = by_word.astype(ml_dtypes.float4_e2m1fn).view(np.uint8) & 0xF
        words = c[..., 0::2] | (c[..., 1::2] << 4)
    return np.ascontiguousarray(words), np.ascontiguousarray(byte.astype(np.uint8).reshape(k // 512, 16, n))


def unpack_weight(words, scales, fmt):
    g, p, n, _ = words.shape
    if fmt == "e4m3":
        vals = np.ascontiguousarray(words).view(ml_dtypes.float8_e4m3fn).astype(np.float64)
    else:
        nib = np.empty((g, p, n, 4), np.uint8)
        nib[..., 0::2] = words & 0xF
        nib[..., 1::2] = words >> 4
        vals = E2M1[nib]
    vals = vals * np.repeat(np.exp2(scales.astype(np.float64) - 127.0), 8, axis=1)[..., None]
    return vals.transpose(0, 1, 3, 2).reshape(g * 512, n)


B, H, L, G, P = 128, 1024, 4, 4, 2


def sigmoid(v):
    return 1.0 / (1.0 + np.exp(-v))


def setup_inputs():
    sc = 1.0 / np.sqrt(H)
    th = np.stack([mx_kscale(H) for _ in range(P)], axis=-1)
    si = np.ones((P, H))
    si[0] = mx_kscale(H)
    lstm_input = bf(np.random.standard_normal((B, H)) * 0.3 * si[0])
    h0 = bf(np.random.standard_normal((B, H, P)) * th)
    c0 = bf(np.random.standard_normal((B, H, P)))
    w_ih = np.random.standard_normal((P, G * H, H)) * sc / si[:, None, :]
    w_hh = np.random.standard_normal((P, G * H, H)) * sc / th.T[:, None, :]
    b_ih = bf(np.random.standard_normal((P, G * H)) * 0.3)
    b_hh = bf(np.random.standard_normal((P, G * H)) * 0.3)
    ih_words, ih_scales = pack_weight(np.ascontiguousarray(w_ih.swapaxes(1, 2)).reshape(-1, G * H), "e4m3")
    hh_words, hh_scales = pack_weight(np.ascontiguousarray(w_hh.swapaxes(1, 2)).reshape(-1, G * H), "e4m3")
    return {"lstm_input": lstm_input,
            "h0": h0,
            "c0": c0,
            "W_ih_words": ih_words,
            "W_ih_scales": ih_scales,
            "W_hh_words": hh_words,
            "W_hh_scales": hh_scales,
            "b_ih": b_ih,
            "b_hh": b_hh}


def reference(lstm_input, h0, c0, W_ih_words, W_ih_scales, W_hh_words, W_hh_scales, b_ih, b_hh):
    inp = f64(lstm_input)
    h0, c0 = f64(h0), f64(c0)
    b_ih, b_hh = f64(b_ih), f64(b_hh)
    W_ih_t = unpack_weight(W_ih_words, W_ih_scales, "e4m3").reshape(P, H, G * H)
    W_hh_t = unpack_weight(W_hh_words, W_hh_scales, "e4m3").reshape(P, H, G * H)
    hs, cs = [], []
    for j in range(P):
        gates = ((mxq(inp, 1, "e4m3") @ W_ih_t[j]) + b_ih[j]
                 + (mxq(h0[:, :, j], 1, "e4m3") @ W_hh_t[j]) + b_hh[j])
        i, f, g, o = np.split(gates, G, axis=-1)
        i = sigmoid(i)
        f = sigmoid(f)
        g = np.tanh(g)
        o = sigmoid(o)
        c_j = f * c0[:, :, j] + i * g
        h_j = o * np.tanh(c_j)
        inp = h_j
        hs.append(h_j)
        cs.append(c_j)
    return np.stack(hs, axis=-1), np.stack(cs, axis=-1)

@@ -1,0 +1,200 @@
+from contextlib import ExitStack
+
+import concourse.mybir as mybir
+from concourse.masks import make_identity
+
+F32 = mybir.dt.float32
+BF16 = mybir.dt.bfloat16
+I32 = mybir.dt.int32
+U32 = mybir.dt.uint32
+U8 = mybir.dt.uint8
+FP8X4 = mybir.dt.float8_e4m3fn_x4
+ACT = mybir.ActivationFunctionType
+ALU = mybir.AluOpType
+
+P = 128
+PACK = 4
+K_PASS = P * PACK
+H = 1024
+LAYERS = 2
+PASSES = H // K_PASS
+BANK = 512
+HALVES = H // BANK
+QUADRANTS = 4
+LIVE = 4
+
+GATE_I, GATE_F, GATE_G, GATE_O = 0, 1, 2, 3
+GATES = 4
+GATE_ORDER = (GATE_I, GATE_G, GATE_F, GATE_O)
+SOURCES = (("ih", "hh"), ("hh", "ih"))
+
+assert BANK == K_PASS
+
+FLOPS = 2 * P * (2 * H) * (GATES * H) * LAYERS
+
+
+def tile_multilayerlstmcell_pb_e_kernel(
+    tc, lstm_input, h0, c0, W_ih_words, W_ih_scales, W_hh_words, W_hh_scales, b_ih, b_hh, out_0, out_1
+):
+    nc = tc.nc
+    words_in_hbm = {"ih": W_ih_words, "hh": W_hh_words}
+    scales_in_hbm = {"ih": W_ih_scales, "hh": W_hh_scales}
+
+    with ExitStack() as stack:
+        keep = stack.enter_context(tc.tile_pool(name="keep", bufs=1))
+        work = stack.enter_context(tc.tile_pool(name="work", bufs=2))
+        leave = stack.enter_context(tc.tile_pool(name="leave", bufs=2 * HALVES))
+        banks = stack.enter_context(tc.psum_pool(name="banks", bufs=6))
+        flips = stack.enter_context(tc.psum_pool(name="flips", bufs=2))
+
+        bias_rows = keep.tile([P, BANK], BF16)
+        nc.vector.memset(bias_rows[:], 0.0)
+        w_scales = {}
+        for source in ("ih", "hh"):
+            w_scales[source] = keep.tile([P, GATES * H], U8, name="w_scales_" + source, align_bytes=64)
+            nc.vector.memset(w_scales[source][:].bitcast(I32), 0)
+
+        x_sb = keep.tile([P, H], BF16)
+        h0_sb = keep.tile([P, H, LAYERS], BF16)
+        c0_sb = keep.tile([P, H, LAYERS], BF16)
+        nc.sync.dma_start(out=x_sb[:], in_=lstm_input)
+        nc.sync.dma_start(out=h0_sb[:], in_=h0)
+        nc.sync.dma_start(out=c0_sb[:], in_=c0)
+        blocks = LAYERS * GATES * HALVES
+        nc.sync.dma_start(out=bias_rows[0:blocks, :], in_=b_ih.rearrange("j (c n) -> (j c) n", n=BANK))
+        nc.sync.dma_start(out=bias_rows[blocks : 2 * blocks, :], in_=b_hh.rearrange("j (c n) -> (j c) n", n=BANK))
+        for source in ("ih", "hh"):
+            for quadrant in range(QUADRANTS):
+                nc.sync.dma_start(
+                    out=w_scales[source][32 * quadrant : 32 * quadrant + 4 * LIVE, :].bitcast(I32),
+                    in_=scales_in_hbm[source][:, LIVE * quadrant : LIVE * (quadrant + 1), :].bitcast(I32),
+                )
+        w_words = {}
+        for layer in range(LAYERS):
+            for gate in GATE_ORDER:
+                for source in SOURCES[layer]:
+                    for kpass in range(PASSES):
+                        group = PASSES * layer + kpass
+                        chunk = keep.tile([P, H], U32, name="w_%s_%d_%d" % (source, group, gate), align_bytes=64)
+                        row_bytes = words_in_hbm[source][group].rearrange("p n t -> p (n t)")
+                        nc.sync.dma_start(
+                            out=chunk[:].bitcast(I32),
+                            in_=row_bytes[:, PACK * H * gate : PACK * H * (gate + 1)].bitcast(I32),
+                        )
+                        w_words[(source, group, gate)] = chunk
+
+        ident = keep.tile([P, P], BF16)
+        make_identity(nc, ident[:])
+
+        a_words = {}
+        a_scales = {}
+        for layer in range(LAYERS):
+            for source in ("ih", "hh"):
+                a_words[(source, layer)] = keep.tile(
+                    [P, PASSES, P], U32, name="a_words_%s%d" % (source, layer), align_bytes=64
+                )
+                a_scales[(source, layer)] = keep.tile(
+                    [P, PASSES, P], U8, name="a_scales_%s%d" % (source, layer), align_bytes=64
+                )
+
+        def quantise_pass(rows, operand, kpass):
+            sorted_k = work.tile([P, PACK, P], BF16)
+            nc.scalar.copy(out=sorted_k[:], in_=rows.rearrange("r (q t) -> r t q", t=PACK))
+            flipped = flips.tile([P, PACK, P], BF16)
+            for t in range(PACK):
+                nc.tensor.transpose(flipped[:, t, :], sorted_k[:, t, :], ident[:])
+            grouped = work.tile([P, P, PACK], BF16, align_bytes=64)
+            nc.vector.tensor_copy(out=grouped[:], in_=flipped[:].rearrange("q t r -> q r t"))
+            nc.vector.quantize_mx(
+                out=a_words[operand][:, kpass, :].bitcast(FP8X4),
+                scales=a_scales[operand][:, kpass, :],
+                in_=grouped[:].rearrange("q r t -> q (r t)"),
+            )
+
+        for kpass in range(PASSES):
+            quantise_pass(x_sb[:, K_PASS * kpass : K_PASS * (kpass + 1)], ("ih", 0), kpass)
+        for layer in range(LAYERS):
+            for kpass in range(PASSES):
+                quantise_pass(h0_sb[:, K_PASS * kpass : K_PASS * (kpass + 1), layer], ("hh", layer), kpass)
+
+        pick = keep.tile([P, blocks], BF16)
+        nc.vector.tensor_tensor(out=pick[:], in0=ident[:, 0:blocks], in1=ident[:, blocks : 2 * blocks], op=ALU.add)
+        gates = [keep.tile([P, GATES, H], F32, name="gates%d" % layer) for layer in range(LAYERS)]
+        for layer in range(LAYERS):
+            for gate in GATE_ORDER:
+                for half in range(HALVES):
+                    block = (layer * GATES + gate) * HALVES + half
+                    spread = banks.tile([P, BANK], F32, tag="bank")
+                    nc.tensor.matmul(
+                        out=spread[:],
+                        lhsT=pick[:, block : block + 1].to_broadcast([P, P]),
+                        rhs=bias_rows[:],
+                        start=True,
+                        stop=True,
+                    )
+                    target = gates[layer][:, gate, BANK * half : BANK * (half + 1)]
+                    if half == 0:
+                        nc.vector.tensor_copy(out=target, in_=spread[:])
+                    else:
+                        nc.scalar.copy(out=target, in_=spread[:])
+
+        cell = keep.tile([P, LAYERS, H], F32)
+        hidden = keep.tile([P, LAYERS, H], F32)
+
+        def gate_values(layer, gate, func):
+            sums = [banks.tile([P, BANK], F32, name="sums%d" % half, tag="bank") for half in range(HALVES)]
+            steps = [(source, kpass) for source in SOURCES[layer] for kpass in range(PASSES)]
+            for step, (source, kpass) in enumerate(steps):
+                group = PASSES * layer + kpass
+                for half in range(HALVES):
+                    nc.tensor.matmul_mx(
+                        out=sums[half][:],
+                        lhsT=a_words[(source, layer)][:, kpass, :].bitcast(FP8X4),
+                        lhsT_scale=a_scales[(source, layer)][:, kpass, :],
+                        rhs=w_words[(source, group, gate)][:, BANK * half : BANK * (half + 1)].bitcast(FP8X4),
+                        rhs_scale=w_scales[source][
+                            LIVE * group : P, H * gate + BANK * half : H * gate + BANK * (half + 1)
+                        ],
+                        start=(step == 0),
+                        stop=(step == len(steps) - 1),
+                    )
+            for half in range(HALVES):
+                values = gates[layer][:, gate, BANK * half : BANK * (half + 1)]
+                nc.vector.tensor_tensor(out=values, in0=sums[half][:], in1=values, op=ALU.add)
+                nc.scalar.activation(out=values, in_=values, func=func)
+
+        def store_states(planes, out):
+            for half in range(HALVES):
+                cols = slice(BANK * half, BANK * (half + 1))
+                both = leave.tile([P, BANK, LAYERS], F32)
+                nc.vector.tensor_copy(out=both[:], in_=planes[:, :, cols].rearrange("p j n -> p n j"))
+                nc.sync.dma_start(out=out[:, cols, :], in_=both[:])
+
+        for layer in range(LAYERS):
+            gate_values(layer, GATE_I, ACT.Sigmoid)
+            gate_values(layer, GATE_G, ACT.Tanh)
+            for half in range(HALVES):
+                cols = slice(BANK * half, BANK * (half + 1))
+                i_g = gates[layer][:, GATE_I, cols]
+                nc.vector.tensor_tensor(out=i_g, in0=i_g, in1=gates[layer][:, GATE_G, cols], op=ALU.mult)
+            gate_values(layer, GATE_F, ACT.Sigmoid)
+            for half in range(HALVES):
+                cols = slice(BANK * half, BANK * (half + 1))
+                f_c = gates[layer][:, GATE_F, cols]
+                nc.vector.tensor_tensor(out=f_c, in0=f_c, in1=c0_sb[:, cols, layer], op=ALU.mult)
+                nc.vector.tensor_tensor(out=cell[:, layer, cols], in0=f_c, in1=gates[layer][:, GATE_I, cols], op=ALU.add)
+                nc.scalar.activation(out=gates[layer][:, GATE_G, cols], in_=cell[:, layer, cols], func=ACT.Tanh)
+            if layer == LAYERS - 1:
+                store_states(cell, out_1)
+            gate_values(layer, GATE_O, ACT.Sigmoid)
+            for half in range(HALVES):
+                cols = slice(BANK * half, BANK * (half + 1))
+                nc.vector.tensor_tensor(
+                    out=hidden[:, layer, cols],
+                    in0=gates[layer][:, GATE_O, cols],
+                    in1=gates[layer][:, GATE_G, cols],
+                    op=ALU.mult,
+                )
+                if layer + 1 < LAYERS:
+                    quantise_pass(hidden[:, layer, cols], ("ih", layer + 1), half)
+        store_states(hidden, out_0)

@@ -65,9 +65,9 @@ def tile_multilayerlstmcell_pb_e_kernel(
         nc.sync.dma_start(out=bias_rows[blocks : 2 * blocks, :], in_=b_hh.rearrange("j (c n) -> (j c) n", n=BANK))
         for source in ("ih", "hh"):
             for quadrant in range(QUADRANTS):
-                nc.sync.dma_start(
-                    out=w_scales[source][32 * quadrant : 32 * quadrant + 4 * LIVE, :].bitcast(I32),
-                    in_=scales_in_hbm[source][:, LIVE * quadrant : LIVE * (quadrant + 1), :].bitcast(I32),
+                nc.gpsimd.dma_start(
+                    out=w_scales[source][32 * quadrant : 32 * quadrant + 4 * LIVE, :].bitcast(F32),
+                    in_=scales_in_hbm[source][:, LIVE * quadrant : LIVE * (quadrant + 1), :].bitcast(F32),
                 )
         w_words = {}
         for layer in range(LAYERS):

@@ -25,7 +25,8 @@ LIVE = 4
 
 GATE_I, GATE_F, GATE_G, GATE_O = 0, 1, 2, 3
 GATES = 4
-GATE_ORDER = (GATE_I, GATE_G, GATE_F, GATE_O)
+GATE_FUNC = {GATE_I: ACT.Sigmoid, GATE_F: ACT.Sigmoid, GATE_G: ACT.Tanh, GATE_O: ACT.Sigmoid}
+STAGES = ((GATE_I, GATE_F), (GATE_G,), (GATE_O,))
 SOURCES = (("ih", "hh"), ("hh", "ih"))
 
 assert BANK == K_PASS
@@ -65,23 +66,31 @@ def tile_multilayerlstmcell_pb_e_kernel(
         nc.sync.dma_start(out=bias_rows[blocks : 2 * blocks, :], in_=b_hh.rearrange("j (c n) -> (j c) n", n=BANK))
         for source in ("ih", "hh"):
             for quadrant in range(QUADRANTS):
-                nc.gpsimd.dma_start(
-                    out=w_scales[source][32 * quadrant : 32 * quadrant + 4 * LIVE, :].bitcast(F32),
-                    in_=scales_in_hbm[source][:, LIVE * quadrant : LIVE * (quadrant + 1), :].bitcast(F32),
+                nc.sync.dma_start(
+                    out=w_scales[source][32 * quadrant : 32 * quadrant + 4 * LIVE, :].bitcast(I32),
+                    in_=scales_in_hbm[source][:, LIVE * quadrant : LIVE * (quadrant + 1), :].bitcast(I32),
                 )
+        loads = [
+            (layer, stage, source, kpass)
+            for layer in range(LAYERS)
+            for stage in STAGES
+            for source in SOURCES[layer]
+            for kpass in range(PASSES)
+        ]
         w_words = {}
-        for layer in range(LAYERS):
-            for gate in GATE_ORDER:
-                for source in SOURCES[layer]:
-                    for kpass in range(PASSES):
-                        group = PASSES * layer + kpass
-                        chunk = keep.tile([P, H], U32, name="w_%s_%d_%d" % (source, group, gate), align_bytes=64)
-                        row_bytes = words_in_hbm[source][group].rearrange("p n t -> p (n t)")
-                        nc.sync.dma_start(
-                            out=chunk[:].bitcast(I32),
-                            in_=row_bytes[:, PACK * H * gate : PACK * H * (gate + 1)].bitcast(I32),
-                        )
-                        w_words[(source, group, gate)] = chunk
+        for index, (layer, stage, source, kpass) in enumerate(loads):
+            group = PASSES * layer + kpass
+            width = H * len(stage)
+            chunk = keep.tile([P, width], U32, name="w_%s_%d_%d" % (source, group, stage[0]), align_bytes=64)
+            row_words = words_in_hbm[source][group].rearrange("p n t -> p (n t)").bitcast(I32)
+            piece = BANK if index == len(loads) - 1 else width
+            for start in range(0, width, piece):
+                nc.sync.dma_start(
+                    out=chunk[:, start : start + piece].bitcast(I32),
+                    in_=row_words[:, H * stage[0] + start : H * stage[0] + start + piece],
+                )
+            for place, gate in enumerate(stage):
+                w_words[(source, group, gate)] = chunk[:, H * place : H * (place + 1)]
 
         ident = keep.tile([P, P], BF16)
         make_identity(nc, ident[:])
@@ -121,7 +130,7 @@ def tile_multilayerlstmcell_pb_e_kernel(
         nc.vector.tensor_tensor(out=pick[:], in0=ident[:, 0:blocks], in1=ident[:, blocks : 2 * blocks], op=ALU.add)
         gates = [keep.tile([P, GATES, H], F32, name="gates%d" % layer) for layer in range(LAYERS)]
         for layer in range(LAYERS):
-            for gate in GATE_ORDER:
+            for gate in range(GATES):
                 for half in range(HALVES):
                     block = (layer * GATES + gate) * HALVES + half
                     spread = banks.tile([P, BANK], F32, tag="bank")
@@ -140,61 +149,77 @@ def tile_multilayerlstmcell_pb_e_kernel(
 
         cell = keep.tile([P, LAYERS, H], F32)
         hidden = keep.tile([P, LAYERS, H], F32)
+        half_cols = [slice(BANK * half, BANK * (half + 1)) for half in range(HALVES)]
 
-        def gate_values(layer, gate, func):
-            sums = [banks.tile([P, BANK], F32, name="sums%d" % half, tag="bank") for half in range(HALVES)]
+        def stage_sums(layer, stage):
+            sums = {}
+            for gate in stage:
+                for half in range(HALVES):
+                    sums[(gate, half)] = banks.tile([P, BANK], F32, name="sums_%d_%d" % (gate, half), tag="bank")
             steps = [(source, kpass) for source in SOURCES[layer] for kpass in range(PASSES)]
             for step, (source, kpass) in enumerate(steps):
                 group = PASSES * layer + kpass
-                for half in range(HALVES):
-                    nc.tensor.matmul_mx(
-                        out=sums[half][:],
-                        lhsT=a_words[(source, layer)][:, kpass, :].bitcast(FP8X4),
-                        lhsT_scale=a_scales[(source, layer)][:, kpass, :],
-                        rhs=w_words[(source, group, gate)][:, BANK * half : BANK * (half + 1)].bitcast(FP8X4),
-                        rhs_scale=w_scales[source][
-                            LIVE * group : P, H * gate + BANK * half : H * gate + BANK * (half + 1)
-                        ],
-                        start=(step == 0),
-                        stop=(step == len(steps) - 1),
-                    )
-            for half in range(HALVES):
-                values = gates[layer][:, gate, BANK * half : BANK * (half + 1)]
-                nc.vector.tensor_tensor(out=values, in0=sums[half][:], in1=values, op=ALU.add)
-                nc.scalar.activation(out=values, in_=values, func=func)
+                for gate in stage:
+                    for half in range(HALVES):
+                        nc.tensor.matmul_mx(
+                            out=sums[(gate, half)][:],
+                            lhsT=a_words[(source, layer)][:, kpass, :].bitcast(FP8X4),
+                            lhsT_scale=a_scales[(source, layer)][:, kpass, :],
+                            rhs=w_words[(source, group, gate)][:, half_cols[half]].bitcast(FP8X4),
+                            rhs_scale=w_scales[source][
+                                LIVE * group : P, H * gate + BANK * half : H * gate + BANK * (half + 1)
+                            ],
+                            start=(step == 0),
+                            stop=(step == len(steps) - 1),
+                        )
+            return sums
 
-        def store_states(planes, out):
-            for half in range(HALVES):
-                cols = slice(BANK * half, BANK * (half + 1))
-                both = leave.tile([P, BANK, LAYERS], F32)
-                nc.vector.tensor_copy(out=both[:], in_=planes[:, :, cols].rearrange("p j n -> p n j"))
-                nc.sync.dma_start(out=out[:, cols, :], in_=both[:])
+        def vector_copy(out, in_):
+            nc.vector.tensor_copy(out=out, in_=in_)
+
+        def gpsimd_copy(out, in_):
+            nc.gpsimd.tensor_scalar(out=out, in0=in_, scalar1=1.0, scalar2=0.0, op0=ALU.mult, op1=ALU.add)
+
+        def store_half(copy, planes, out, half):
+            both = leave.tile([P, BANK, LAYERS], F32)
+            copy(both[:], planes[:, :, half_cols[half]].rearrange("p j n -> p n j"))
+            nc.sync.dma_start(out=out[:, half_cols[half], :], in_=both[:])
 
         for layer in range(LAYERS):
-            gate_values(layer, GATE_I, ACT.Sigmoid)
-            gate_values(layer, GATE_G, ACT.Tanh)
-            for half in range(HALVES):
-                cols = slice(BANK * half, BANK * (half + 1))
-                i_g = gates[layer][:, GATE_I, cols]
-                nc.vector.tensor_tensor(out=i_g, in0=i_g, in1=gates[layer][:, GATE_G, cols], op=ALU.mult)
-            gate_values(layer, GATE_F, ACT.Sigmoid)
-            for half in range(HALVES):
-                cols = slice(BANK * half, BANK * (half + 1))
-                f_c = gates[layer][:, GATE_F, cols]
-                nc.vector.tensor_tensor(out=f_c, in0=f_c, in1=c0_sb[:, cols, layer], op=ALU.mult)
-                nc.vector.tensor_tensor(out=cell[:, layer, cols], in0=f_c, in1=gates[layer][:, GATE_I, cols], op=ALU.add)
-                nc.scalar.activation(out=gates[layer][:, GATE_G, cols], in_=cell[:, layer, cols], func=ACT.Tanh)
-            if layer == LAYERS - 1:
-                store_states(cell, out_1)
-            gate_values(layer, GATE_O, ACT.Sigmoid)
-            for half in range(HALVES):
-                cols = slice(BANK * half, BANK * (half + 1))
-                nc.vector.tensor_tensor(
-                    out=hidden[:, layer, cols],
-                    in0=gates[layer][:, GATE_O, cols],
-                    in1=gates[layer][:, GATE_G, cols],
-                    op=ALU.mult,
-                )
-                if layer + 1 < LAYERS:
+            last_layer = layer == LAYERS - 1
+            value = {gate: gates[layer][:, gate, :] for gate in range(GATES)}
+            for stage in STAGES:
+                sums = stage_sums(layer, stage)
+                for gate in stage:
+                    for half, cols in enumerate(half_cols):
+                        nc.vector.tensor_tensor(
+                            out=value[gate][:, cols], in0=sums[(gate, half)][:], in1=value[gate][:, cols], op=ALU.add
+                        )
+                        nc.scalar.activation(out=value[gate][:, cols], in_=value[gate][:, cols], func=GATE_FUNC[gate])
+                if GATE_F in stage:
+                    for cols in half_cols:
+                        nc.vector.tensor_tensor(
+                            out=value[GATE_F][:, cols], in0=value[GATE_F][:, cols], in1=c0_sb[:, cols, layer], op=ALU.mult
+                        )
+                if GATE_G in stage:
+                    for cols in half_cols:
+                        nc.vector.tensor_tensor(
+                            out=value[GATE_I][:, cols], in0=value[GATE_I][:, cols], in1=value[GATE_G][:, cols], op=ALU.mult
+                        )
+                        nc.vector.tensor_tensor(
+                            out=cell[:, layer, cols], in0=value[GATE_F][:, cols], in1=value[GATE_I][:, cols], op=ALU.add
+                        )
+                        nc.scalar.activation(out=value[GATE_G][:, cols], in_=cell[:, layer, cols], func=ACT.Tanh)
+                    if last_layer:
+                        for half in range(HALVES):
+                            store_half(gpsimd_copy, cell, out_1, half)
+                if GATE_O in stage:
+                    for half, cols in enumerate(half_cols):
+                        nc.vector.tensor_tensor(
+                            out=hidden[:, layer, cols], in0=value[GATE_O][:, cols], in1=value[GATE_G][:, cols], op=ALU.mult
+                        )
+                        if last_layer:
+                            store_half(vector_copy, hidden, out_0, half)
+            if not last_layer:
+                for half, cols in enumerate(half_cols):
                     quantise_pass(hidden[:, layer, cols], ("ih", layer + 1), half)
-        store_states(hidden, out_0)

@@ -26,8 +26,7 @@ LIVE = 4
 GATE_I, GATE_F, GATE_G, GATE_O = 0, 1, 2, 3
 GATES = 4
 GATE_FUNC = {GATE_I: ACT.Sigmoid, GATE_F: ACT.Sigmoid, GATE_G: ACT.Tanh, GATE_O: ACT.Sigmoid}
-STAGES = ((GATE_I, GATE_F), (GATE_G,), (GATE_O,))
-SOURCES = (("ih", "hh"), ("hh", "ih"))
+CELL_GATES = (GATE_I, GATE_F, GATE_G)
 
 assert BANK == K_PASS
 
@@ -40,60 +39,86 @@ def tile_multilayerlstmcell_pb_e_kernel(
     nc = tc.nc
     words_in_hbm = {"ih": W_ih_words, "hh": W_hh_words}
     scales_in_hbm = {"ih": W_ih_scales, "hh": W_hh_scales}
+    half_cols = [slice(BANK * half, BANK * (half + 1)) for half in range(HALVES)]
 
     with ExitStack() as stack:
         keep = stack.enter_context(tc.tile_pool(name="keep", bufs=1))
         work = stack.enter_context(tc.tile_pool(name="work", bufs=2))
-        leave = stack.enter_context(tc.tile_pool(name="leave", bufs=2 * HALVES))
-        banks = stack.enter_context(tc.psum_pool(name="banks", bufs=6))
-        flips = stack.enter_context(tc.psum_pool(name="flips", bufs=2))
+        banks = stack.enter_context(tc.psum_pool(name="banks", bufs=8))
 
-        bias_rows = keep.tile([P, BANK], BF16)
-        nc.vector.memset(bias_rows[:], 0.0)
         w_scales = {}
         for source in ("ih", "hh"):
             w_scales[source] = keep.tile([P, GATES * H], U8, name="w_scales_" + source, align_bytes=64)
             nc.vector.memset(w_scales[source][:].bitcast(I32), 0)
+        bias_rows = keep.tile([P, BANK], BF16)
+        nc.vector.memset(bias_rows[:], 0.0)
 
         x_sb = keep.tile([P, H], BF16)
         h0_sb = keep.tile([P, H, LAYERS], BF16)
         c0_sb = keep.tile([P, H, LAYERS], BF16)
-        nc.sync.dma_start(out=x_sb[:], in_=lstm_input)
-        nc.sync.dma_start(out=h0_sb[:], in_=h0)
-        nc.sync.dma_start(out=c0_sb[:], in_=c0)
-        blocks = LAYERS * GATES * HALVES
-        nc.sync.dma_start(out=bias_rows[0:blocks, :], in_=b_ih.rearrange("j (c n) -> (j c) n", n=BANK))
-        nc.sync.dma_start(out=bias_rows[blocks : 2 * blocks, :], in_=b_hh.rearrange("j (c n) -> (j c) n", n=BANK))
-        for source in ("ih", "hh"):
+        w_words = {}
+
+        def load_scales(source):
             for quadrant in range(QUADRANTS):
                 nc.sync.dma_start(
                     out=w_scales[source][32 * quadrant : 32 * quadrant + 4 * LIVE, :].bitcast(I32),
                     in_=scales_in_hbm[source][:, LIVE * quadrant : LIVE * (quadrant + 1), :].bitcast(I32),
                 )
-        loads = [
-            (layer, stage, source, kpass)
-            for layer in range(LAYERS)
-            for stage in STAGES
-            for source in SOURCES[layer]
-            for kpass in range(PASSES)
-        ]
-        w_words = {}
-        for index, (layer, stage, source, kpass) in enumerate(loads):
-            group = PASSES * layer + kpass
-            width = H * len(stage)
-            chunk = keep.tile([P, width], U32, name="w_%s_%d_%d" % (source, group, stage[0]), align_bytes=64)
+
+        def load_group(source, group, gates_loaded):
+            width = H * len(gates_loaded)
+            first = H * gates_loaded[0]
+            chunk = keep.tile([P, width], U32, name="w_%s_%d_%d" % (source, group, gates_loaded[0]), align_bytes=64)
             row_words = words_in_hbm[source][group].rearrange("p n t -> p (n t)").bitcast(I32)
-            piece = BANK if index == len(loads) - 1 else width
-            for start in range(0, width, piece):
-                nc.sync.dma_start(
-                    out=chunk[:, start : start + piece].bitcast(I32),
-                    in_=row_words[:, H * stage[0] + start : H * stage[0] + start + piece],
-                )
-            for place, gate in enumerate(stage):
+            nc.sync.dma_start(out=chunk[:].bitcast(I32), in_=row_words[:, first : first + width])
+            for place, gate in enumerate(gates_loaded):
                 w_words[(source, group, gate)] = chunk[:, H * place : H * (place + 1)]
+
+        gate_tiles = {}
+
+        def load_gate(source, layer, gate, pieces):
+            first_group = PASSES * layer
+            if (source, layer, gate) not in gate_tiles:
+                chunk = keep.tile([P, PASSES, H], U32, name="w_%s_%d_%d" % (source, first_group, gate), align_bytes=64)
+                gate_tiles[(source, layer, gate)] = chunk
+                for kpass in range(PASSES):
+                    w_words[(source, first_group + kpass, gate)] = chunk[:, kpass, :]
+            row_words = (
+                words_in_hbm[source][first_group : first_group + PASSES].rearrange("g p n t -> p g (n t)").bitcast(I32)
+            )
+            for cols in pieces:
+                nc.sync.dma_start(
+                    out=gate_tiles[(source, layer, gate)][:, :, cols].bitcast(I32),
+                    in_=row_words[:, :, H * gate + cols.start : H * gate + cols.stop],
+                )
+
+        blocks = LAYERS * GATES * HALVES
+        nc.sync.dma_start(out=x_sb[:], in_=lstm_input)
+        nc.sync.dma_start(out=bias_rows[0:blocks, :], in_=b_ih.rearrange("j (c n) -> (j c) n", n=BANK))
+        nc.sync.dma_start(out=bias_rows[blocks : 2 * blocks, :], in_=b_hh.rearrange("j (c n) -> (j c) n", n=BANK))
+        nc.sync.dma_start(out=h0_sb[:], in_=h0)
+        load_group("ih", 0, CELL_GATES)
+        load_scales("ih")
+        load_group("ih", 1, CELL_GATES)
+        load_scales("hh")
+        load_group("hh", 0, CELL_GATES)
+        nc.sync.dma_start(out=c0_sb[:], in_=c0)
+        load_group("hh", 1, CELL_GATES)
+        for source in ("ih", "hh"):
+            load_gate(source, 0, GATE_O, (slice(0, H),))
+        for kpass in range(PASSES):
+            load_group("hh", PASSES + kpass, CELL_GATES)
+        for gate in (GATE_F, GATE_I):
+            load_gate("ih", 1, gate, (slice(0, H),))
+        for cols in half_cols:
+            load_gate("ih", 1, GATE_G, (cols,))
+            load_gate("hh", 1, GATE_O, (cols,))
+            load_gate("ih", 1, GATE_O, (cols,))
 
         ident = keep.tile([P, P], BF16)
         make_identity(nc, ident[:])
+        ident_f32 = keep.tile([P, P], F32)
+        make_identity(nc, ident_f32[:])
 
         a_words = {}
         a_scales = {}
@@ -106,31 +131,60 @@ def tile_multilayerlstmcell_pb_e_kernel(
                     [P, PASSES, P], U8, name="a_scales_%s%d" % (source, layer), align_bytes=64
                 )
 
-        def quantise_pass(rows, operand, kpass):
-            sorted_k = work.tile([P, PACK, P], BF16)
-            nc.scalar.copy(out=sorted_k[:], in_=rows.rearrange("r (q t) -> r t q", t=PACK))
-            flipped = flips.tile([P, PACK, P], BF16)
-            for t in range(PACK):
-                nc.tensor.transpose(flipped[:, t, :], sorted_k[:, t, :], ident[:])
-            grouped = work.tile([P, P, PACK], BF16, align_bytes=64)
-            nc.vector.tensor_copy(out=grouped[:], in_=flipped[:].rearrange("q t r -> q r t"))
+        def quantise(grouped, operand, kpass):
             nc.vector.quantize_mx(
                 out=a_words[operand][:, kpass, :].bitcast(FP8X4),
                 scales=a_scales[operand][:, kpass, :],
                 in_=grouped[:].rearrange("q r t -> q (r t)"),
             )
 
-        for kpass in range(PASSES):
-            quantise_pass(x_sb[:, K_PASS * kpass : K_PASS * (kpass + 1)], ("ih", 0), kpass)
-        for layer in range(LAYERS):
-            for kpass in range(PASSES):
-                quantise_pass(h0_sb[:, K_PASS * kpass : K_PASS * (kpass + 1), layer], ("hh", layer), kpass)
+        def quantise_input(kpass):
+            words = x_sb[:].bitcast(F32)
+            flipped = banks.tile([P, 2, P], F32, tag="bank")
+            first = kpass * K_PASS // 2
+            for u in range(2):
+                nc.tensor.transpose(flipped[:, u, :], words[:, first + u : first + K_PASS // 2 : 2], ident_f32[:])
+            grouped = work.tile([P, P, PACK], BF16, align_bytes=64)
+            nc.vector.tensor_copy(
+                out=grouped[:].bitcast(F32), in_=flipped[:].rearrange("q u r -> q r u")
+            )
+            quantise(grouped, ("ih", 0), kpass)
+
+        def quantise_states(kpass):
+            words = h0_sb[:].rearrange("r k j -> r (k j)").bitcast(F32)
+            flipped = banks.tile([P, PACK, P], F32, tag="bank")
+            for t in range(PACK):
+                nc.tensor.transpose(
+                    flipped[:, t, :], words[:, K_PASS * kpass + t : K_PASS * (kpass + 1) : PACK], ident_f32[:]
+                )
+            pairs = flipped[:].bitcast(BF16).rearrange("q t (r j) -> q j r t", j=LAYERS)
+            for layer in range(LAYERS):
+                grouped = work.tile([P, P, PACK], BF16, align_bytes=64)
+                nc.vector.tensor_copy(out=grouped[:], in_=pairs[:, layer])
+                quantise(grouped, ("hh", layer), kpass)
+
+        def quantise_hidden(half):
+            sorted_k = work.tile([P, PACK, P], BF16)
+            cols = half_cols[half]
+            nc.vector.tensor_tensor(
+                out=sorted_k[:],
+                in0=values[:, GATE_O, 0, cols].rearrange("r (q t) -> r t q", t=PACK),
+                in1=values[:, GATE_G, 0, cols].rearrange("r (q t) -> r t q", t=PACK),
+                op=ALU.mult,
+            )
+            flipped = banks.tile([P, PACK, P], BF16, tag="bank")
+            for t in range(PACK):
+                nc.tensor.transpose(flipped[:, t, :], sorted_k[:, t, :], ident[:])
+            grouped = work.tile([P, P, PACK], BF16, align_bytes=64)
+            nc.vector.tensor_copy(out=grouped[:], in_=flipped[:].rearrange("q t r -> q r t"))
+            quantise(grouped, ("ih", 1), half)
 
         pick = keep.tile([P, blocks], BF16)
         nc.vector.tensor_tensor(out=pick[:], in0=ident[:, 0:blocks], in1=ident[:, blocks : 2 * blocks], op=ALU.add)
-        gates = [keep.tile([P, GATES, H], F32, name="gates%d" % layer) for layer in range(LAYERS)]
-        for layer in range(LAYERS):
-            for gate in range(GATES):
+        values = keep.tile([P, GATES, LAYERS, H], F32)
+
+        def spread_biases(layer):
+            for gate in (GATE_F, GATE_I, GATE_G, GATE_O):
                 for half in range(HALVES):
                     block = (layer * GATES + gate) * HALVES + half
                     spread = banks.tile([P, BANK], F32, tag="bank")
@@ -141,85 +195,135 @@ def tile_multilayerlstmcell_pb_e_kernel(
                         start=True,
                         stop=True,
                     )
-                    target = gates[layer][:, gate, BANK * half : BANK * (half + 1)]
+                    target = values[:, gate, layer, half_cols[half]]
                     if half == 0:
                         nc.vector.tensor_copy(out=target, in_=spread[:])
                     else:
                         nc.scalar.copy(out=target, in_=spread[:])
 
-        cell = keep.tile([P, LAYERS, H], F32)
-        hidden = keep.tile([P, LAYERS, H], F32)
-        half_cols = [slice(BANK * half, BANK * (half + 1)) for half in range(HALVES)]
-
-        def stage_sums(layer, stage):
-            sums = {}
-            for gate in stage:
-                for half in range(HALVES):
-                    sums[(gate, half)] = banks.tile([P, BANK], F32, name="sums_%d_%d" % (gate, half), tag="bank")
-            steps = [(source, kpass) for source in SOURCES[layer] for kpass in range(PASSES)]
-            for step, (source, kpass) in enumerate(steps):
-                group = PASSES * layer + kpass
-                for gate in stage:
-                    for half in range(HALVES):
-                        nc.tensor.matmul_mx(
-                            out=sums[(gate, half)][:],
-                            lhsT=a_words[(source, layer)][:, kpass, :].bitcast(FP8X4),
-                            lhsT_scale=a_scales[(source, layer)][:, kpass, :],
-                            rhs=w_words[(source, group, gate)][:, half_cols[half]].bitcast(FP8X4),
-                            rhs_scale=w_scales[source][
-                                LIVE * group : P, H * gate + BANK * half : H * gate + BANK * (half + 1)
-                            ],
-                            start=(step == 0),
-                            stop=(step == len(steps) - 1),
-                        )
-            return sums
-
-        def vector_copy(out, in_):
-            nc.vector.tensor_copy(out=out, in_=in_)
-
-        def gpsimd_copy(out, in_):
-            nc.gpsimd.tensor_scalar(out=out, in0=in_, scalar1=1.0, scalar2=0.0, op0=ALU.mult, op1=ALU.add)
-
-        def store_half(copy, planes, out, half):
-            both = leave.tile([P, BANK, LAYERS], F32)
-            copy(both[:], planes[:, :, half_cols[half]].rearrange("p j n -> p n j"))
-            nc.sync.dma_start(out=out[:, half_cols[half], :], in_=both[:])
-
+        for kpass in range(PASSES):
+            quantise_input(kpass)
+        for kpass in range(PASSES):
+            quantise_states(kpass)
         for layer in range(LAYERS):
-            last_layer = layer == LAYERS - 1
-            value = {gate: gates[layer][:, gate, :] for gate in range(GATES)}
-            for stage in STAGES:
-                sums = stage_sums(layer, stage)
-                for gate in stage:
-                    for half, cols in enumerate(half_cols):
-                        nc.vector.tensor_tensor(
-                            out=value[gate][:, cols], in0=sums[(gate, half)][:], in1=value[gate][:, cols], op=ALU.add
-                        )
-                        nc.scalar.activation(out=value[gate][:, cols], in_=value[gate][:, cols], func=GATE_FUNC[gate])
-                if GATE_F in stage:
-                    for cols in half_cols:
-                        nc.vector.tensor_tensor(
-                            out=value[GATE_F][:, cols], in0=value[GATE_F][:, cols], in1=c0_sb[:, cols, layer], op=ALU.mult
-                        )
-                if GATE_G in stage:
-                    for cols in half_cols:
-                        nc.vector.tensor_tensor(
-                            out=value[GATE_I][:, cols], in0=value[GATE_I][:, cols], in1=value[GATE_G][:, cols], op=ALU.mult
-                        )
-                        nc.vector.tensor_tensor(
-                            out=cell[:, layer, cols], in0=value[GATE_F][:, cols], in1=value[GATE_I][:, cols], op=ALU.add
-                        )
-                        nc.scalar.activation(out=value[GATE_G][:, cols], in_=cell[:, layer, cols], func=ACT.Tanh)
-                    if last_layer:
-                        for half in range(HALVES):
-                            store_half(gpsimd_copy, cell, out_1, half)
-                if GATE_O in stage:
-                    for half, cols in enumerate(half_cols):
-                        nc.vector.tensor_tensor(
-                            out=hidden[:, layer, cols], in0=value[GATE_O][:, cols], in1=value[GATE_G][:, cols], op=ALU.mult
-                        )
-                        if last_layer:
-                            store_half(vector_copy, hidden, out_0, half)
-            if not last_layer:
-                for half, cols in enumerate(half_cols):
-                    quantise_pass(hidden[:, layer, cols], ("ih", layer + 1), half)
+            spread_biases(layer)
+
+        sums = {}
+
+        def add_pass(layer, source, kpass, gate, half, start, stop):
+            if start:
+                sums[(layer, gate, half)] = banks.tile([P, BANK], F32, name="sums_%d_%d" % (gate, half), tag="bank")
+            group = PASSES * layer + kpass
+            nc.tensor.matmul_mx(
+                out=sums[(layer, gate, half)][:],
+                lhsT=a_words[(source, layer)][:, kpass, :].bitcast(FP8X4),
+                lhsT_scale=a_scales[(source, layer)][:, kpass, :],
+                rhs=w_words[(source, group, gate)][:, half_cols[half]].bitcast(FP8X4),
+                rhs_scale=w_scales[source][LIVE * group : P, H * gate + BANK * half : H * gate + BANK * (half + 1)],
+                start=start,
+                stop=stop,
+            )
+
+        def finish_gate(layer, gate, half, pieces=1):
+            width = BANK // pieces
+            for start in range(0, BANK, width):
+                first = BANK * half + start
+                value = values[:, gate, layer, first : first + width]
+                nc.vector.tensor_tensor(
+                    out=value, in0=sums[(layer, gate, half)][:, start : start + width], in1=value, op=ALU.add
+                )
+                nc.scalar.activation(out=value, in_=value, func=GATE_FUNC[gate])
+
+        def times(engine, gate, other, layer, half):
+            value = values[:, gate, layer, half_cols[half]]
+            engine.tensor_tensor(out=value, in0=value, in1=other, op=ALU.mult)
+
+        cells = keep.tile([P, LAYERS, H], F32)
+
+        def new_cell(layer, half):
+            cols = half_cols[half]
+            times(nc.vector, GATE_I, values[:, GATE_G, layer, cols], layer, half)
+            nc.vector.tensor_tensor(
+                out=cells[:, layer, cols], in0=values[:, GATE_F, layer, cols], in1=values[:, GATE_I, layer, cols], op=ALU.add
+            )
+            nc.scalar.activation(out=values[:, GATE_G, layer, cols], in_=cells[:, layer, cols], func=ACT.Tanh)
+
+        steps = [(source, kpass) for source in ("ih", "hh") for kpass in range(PASSES)]
+        def lower_sums(gates_summed):
+            for step, (source, kpass) in enumerate(steps):
+                for gate in gates_summed:
+                    for half in range(HALVES):
+                        add_pass(0, source, kpass, gate, half, start=(step == 0), stop=(step == len(steps) - 1))
+
+        lower_sums((GATE_F, GATE_I, GATE_G))
+        for half, cols in enumerate(half_cols):
+            finish_gate(0, GATE_F, half)
+            times(nc.gpsimd, GATE_F, c0_sb[:, cols, 0], 0, half)
+        for gate in (GATE_I, GATE_G):
+            for half in range(HALVES):
+                finish_gate(0, gate, half)
+        for half in range(HALVES):
+            new_cell(0, half)
+        lower_sums((GATE_O,))
+        for half, cols in enumerate(half_cols):
+            finish_gate(0, GATE_O, half)
+
+        def upper_hh(kpass, gates_summed):
+            for gate in gates_summed:
+                for half in range(HALVES):
+                    add_pass(1, "hh", kpass, gate, half, start=(kpass == 0), stop=False)
+
+        upper_hh(0, (GATE_F, GATE_I, GATE_G))
+        for half in range(HALVES):
+            quantise_hidden(half)
+
+        def close_gate(gate, half):
+            if gate == GATE_O:
+                add_pass(1, "hh", 0, gate, half, start=True, stop=False)
+            add_pass(1, "hh", 1, gate, half, start=False, stop=False)
+            for kpass in range(PASSES):
+                add_pass(1, "ih", kpass, gate, half, start=False, stop=(kpass == PASSES - 1))
+
+        cell_out = keep.tile([P, H, LAYERS], F32)
+        hidden_out = keep.tile([P, H, LAYERS], F32)
+
+        def store_cell(half):
+            cols = half_cols[half]
+            nc.scalar.copy(out=cell_out[:, cols, :], in_=cells[:, :, cols].rearrange("p j n -> p n j"))
+            nc.sync.dma_start(out=out_1[:, cols, :], in_=cell_out[:, cols, :])
+
+        def store_hidden(half, pieces=1):
+            width = BANK // pieces
+            for start in range(BANK * half, BANK * (half + 1), width):
+                cols = slice(start, start + width)
+                nc.vector.tensor_tensor(
+                    out=hidden_out[:, cols, :],
+                    in0=values[:, GATE_O, :, cols].rearrange("p j n -> p n j"),
+                    in1=values[:, GATE_G, :, cols].rearrange("p j n -> p n j"),
+                    op=ALU.mult,
+                )
+                nc.sync.dma_start(out=out_0[:, cols, :], in_=hidden_out[:, cols, :])
+
+        engines = {mybir.EngineType.PE, mybir.EngineType.DVE, mybir.EngineType.Activation}
+        with tc.manual_schedule(engines=engines):
+            for half, cols in enumerate(half_cols):
+                close_gate(GATE_F, half)
+                finish_gate(1, GATE_F, half)
+                times(nc.gpsimd, GATE_F, c0_sb[:, cols, 1], 1, half)
+            for half in range(HALVES):
+                close_gate(GATE_I, half)
+                finish_gate(1, GATE_I, half)
+            close_gate(GATE_G, 0)
+            finish_gate(1, GATE_G, 0)
+            new_cell(1, 0)
+            close_gate(GATE_O, 0)
+            finish_gate(1, GATE_O, 0)
+            close_gate(GATE_G, 1)
+            finish_gate(1, GATE_G, 1)
+            store_hidden(0)
+            store_cell(0)
+            new_cell(1, 1)
+            close_gate(GATE_O, 1)
+            finish_gate(1, GATE_O, 1, pieces=2)
+            store_hidden(1, pieces=2)
+            store_cell(1)

@@ -94,13 +94,13 @@ def tile_multilayerlstmcell_pb_e_kernel(
 
         blocks = LAYERS * GATES * HALVES
         nc.sync.dma_start(out=x_sb[:], in_=lstm_input)
+        nc.sync.dma_start(out=h0_sb[:], in_=h0)
         nc.sync.dma_start(out=bias_rows[0:blocks, :], in_=b_ih.rearrange("j (c n) -> (j c) n", n=BANK))
         nc.sync.dma_start(out=bias_rows[blocks : 2 * blocks, :], in_=b_hh.rearrange("j (c n) -> (j c) n", n=BANK))
-        nc.sync.dma_start(out=h0_sb[:], in_=h0)
-        load_group("ih", 0, CELL_GATES)
         load_scales("ih")
-        load_group("ih", 1, CELL_GATES)
         load_scales("hh")
+        for kpass in range(PASSES):
+            load_group("ih", kpass, CELL_GATES)
         load_group("hh", 0, CELL_GATES)
         nc.sync.dma_start(out=c0_sb[:], in_=c0)
         load_group("hh", 1, CELL_GATES)

@@ -26,7 +26,7 @@ LIVE = 4
 GATE_I, GATE_F, GATE_G, GATE_O = 0, 1, 2, 3
 GATES = 4
 GATE_FUNC = {GATE_I: ACT.Sigmoid, GATE_F: ACT.Sigmoid, GATE_G: ACT.Tanh, GATE_O: ACT.Sigmoid}
-CELL_GATES = (GATE_I, GATE_F, GATE_G)
+PAIR = (GATE_I, GATE_F)
 
 assert BANK == K_PASS
 
@@ -58,12 +58,13 @@ def tile_multilayerlstmcell_pb_e_kernel(
         c0_sb = keep.tile([P, H, LAYERS], BF16)
         w_words = {}
 
-        def load_scales(source):
-            for quadrant in range(QUADRANTS):
-                nc.sync.dma_start(
-                    out=w_scales[source][32 * quadrant : 32 * quadrant + 4 * LIVE, :].bitcast(I32),
-                    in_=scales_in_hbm[source][:, LIVE * quadrant : LIVE * (quadrant + 1), :].bitcast(I32),
-                )
+        def load_scales(quadrants):
+            for source in ("ih", "hh"):
+                for quadrant in quadrants:
+                    nc.sync.dma_start(
+                        out=w_scales[source][32 * quadrant : 32 * quadrant + 4 * LIVE, :].bitcast(I32),
+                        in_=scales_in_hbm[source][:, LIVE * quadrant : LIVE * (quadrant + 1), :].bitcast(I32),
+                    )
 
         def load_group(source, group, gates_loaded):
             width = H * len(gates_loaded)
@@ -97,17 +98,18 @@ def tile_multilayerlstmcell_pb_e_kernel(
         nc.sync.dma_start(out=h0_sb[:], in_=h0)
         nc.sync.dma_start(out=bias_rows[0:blocks, :], in_=b_ih.rearrange("j (c n) -> (j c) n", n=BANK))
         nc.sync.dma_start(out=bias_rows[blocks : 2 * blocks, :], in_=b_hh.rearrange("j (c n) -> (j c) n", n=BANK))
-        load_scales("ih")
-        load_scales("hh")
-        for kpass in range(PASSES):
-            load_group("ih", kpass, CELL_GATES)
-        load_group("hh", 0, CELL_GATES)
-        nc.sync.dma_start(out=c0_sb[:], in_=c0)
-        load_group("hh", 1, CELL_GATES)
+        load_scales((2, 3))
+        load_scales((0, 1))
         for source in ("ih", "hh"):
-            load_gate(source, 0, GATE_O, (slice(0, H),))
+            for kpass in range(PASSES):
+                load_group(source, kpass, PAIR)
+        nc.sync.dma_start(out=c0_sb[:], in_=c0)
+        for gate in (GATE_G, GATE_O):
+            for source in ("ih", "hh"):
+                load_gate(source, 0, gate, (slice(0, H),))
         for kpass in range(PASSES):
-            load_group("hh", PASSES + kpass, CELL_GATES)
+            load_group("hh", PASSES + kpass, PAIR)
+        load_gate("hh", 1, GATE_G, (slice(0, H),))
         for gate in (GATE_F, GATE_I):
             load_gate("ih", 1, gate, (slice(0, H),))
         for cols in half_cols:
@@ -255,13 +257,15 @@ def tile_multilayerlstmcell_pb_e_kernel(
                     for half in range(HALVES):
                         add_pass(0, source, kpass, gate, half, start=(step == 0), stop=(step == len(steps) - 1))
 
-        lower_sums((GATE_F, GATE_I, GATE_G))
+        lower_sums(PAIR)
         for half, cols in enumerate(half_cols):
             finish_gate(0, GATE_F, half)
             times(nc.gpsimd, GATE_F, c0_sb[:, cols, 0], 0, half)
-        for gate in (GATE_I, GATE_G):
-            for half in range(HALVES):
-                finish_gate(0, gate, half)
+        for half in range(HALVES):
+            finish_gate(0, GATE_I, half)
+        lower_sums((GATE_G,))
+        for half in range(HALVES):
+            finish_gate(0, GATE_G, half)
         for half in range(HALVES):
             new_cell(0, half)
         lower_sums((GATE_O,))
@@ -273,14 +277,17 @@ def tile_multilayerlstmcell_pb_e_kernel(
                 for half in range(HALVES):
                     add_pass(1, "hh", kpass, gate, half, start=(kpass == 0), stop=False)
 
-        upper_hh(0, (GATE_F, GATE_I, GATE_G))
+        upper_hh(0, PAIR)
         for half in range(HALVES):
             quantise_hidden(half)
+        upper_hh(1, PAIR)
+        for kpass in range(PASSES):
+            upper_hh(kpass, (GATE_G,))
 
         def close_gate(gate, half):
             if gate == GATE_O:
-                add_pass(1, "hh", 0, gate, half, start=True, stop=False)
-            add_pass(1, "hh", 1, gate, half, start=False, stop=False)
+                for kpass in range(PASSES):
+                    add_pass(1, "hh", kpass, gate, half, start=(kpass == 0), stop=False)
             for kpass in range(PASSES):
                 add_pass(1, "ih", kpass, gate, half, start=False, stop=(kpass == PASSES - 1))
 

@@ -27,6 +27,7 @@ GATE_I, GATE_F, GATE_G, GATE_O = 0, 1, 2, 3
 GATES = 4
 GATE_FUNC = {GATE_I: ACT.Sigmoid, GATE_F: ACT.Sigmoid, GATE_G: ACT.Tanh, GATE_O: ACT.Sigmoid}
 PAIR = (GATE_I, GATE_F)
+SECOND_PAIR = (GATE_G, GATE_O)
 
 assert BANK == K_PASS
 
@@ -104,18 +105,17 @@ def tile_multilayerlstmcell_pb_e_kernel(
             for kpass in range(PASSES):
                 load_group(source, kpass, PAIR)
         nc.sync.dma_start(out=c0_sb[:], in_=c0)
-        for gate in (GATE_G, GATE_O):
-            for source in ("ih", "hh"):
-                load_gate(source, 0, gate, (slice(0, H),))
+        for source in ("ih", "hh"):
+            for kpass in range(PASSES):
+                load_group(source, kpass, SECOND_PAIR)
         for kpass in range(PASSES):
             load_group("hh", PASSES + kpass, PAIR)
         load_gate("hh", 1, GATE_G, (slice(0, H),))
-        for gate in (GATE_F, GATE_I):
-            load_gate("ih", 1, gate, (slice(0, H),))
-        for cols in half_cols:
-            load_gate("ih", 1, GATE_G, (cols,))
-            load_gate("hh", 1, GATE_O, (cols,))
-            load_gate("ih", 1, GATE_O, (cols,))
+        for kpass in range(PASSES):
+            load_group("ih", PASSES + kpass, PAIR)
+        load_gate("ih", 1, GATE_G, half_cols)
+        load_gate("hh", 1, GATE_O, (slice(0, H),))
+        load_gate("ih", 1, GATE_O, half_cols)
 
         ident = keep.tile([P, P], BF16)
         make_identity(nc, ident[:])
@@ -263,14 +263,12 @@ def tile_multilayerlstmcell_pb_e_kernel(
             times(nc.gpsimd, GATE_F, c0_sb[:, cols, 0], 0, half)
         for half in range(HALVES):
             finish_gate(0, GATE_I, half)
-        lower_sums((GATE_G,))
+        lower_sums(SECOND_PAIR)
         for half in range(HALVES):
             finish_gate(0, GATE_G, half)
         for half in range(HALVES):
-            new_cell(0, half)
-        lower_sums((GATE_O,))
-        for half, cols in enumerate(half_cols):
             finish_gate(0, GATE_O, half)
+            new_cell(0, half)
 
         def upper_hh(kpass, gates_summed):
             for gate in gates_summed:
@@ -284,53 +282,61 @@ def tile_multilayerlstmcell_pb_e_kernel(
         for kpass in range(PASSES):
             upper_hh(kpass, (GATE_G,))
 
-        def close_gate(gate, half):
-            if gate == GATE_O:
-                for kpass in range(PASSES):
-                    add_pass(1, "hh", kpass, gate, half, start=(kpass == 0), stop=False)
+        def add_source(source, gates_summed):
+            for kpass in range(PASSES):
+                for gate in gates_summed:
+                    for half in range(HALVES):
+                        opens = source == "hh" and kpass == 0
+                        closes = source == "ih" and kpass == PASSES - 1
+                        add_pass(1, source, kpass, gate, half, start=opens, stop=closes)
+
+        def close_half(gate, half):
             for kpass in range(PASSES):
                 add_pass(1, "ih", kpass, gate, half, start=False, stop=(kpass == PASSES - 1))
 
         cell_out = keep.tile([P, H, LAYERS], F32)
         hidden_out = keep.tile([P, H, LAYERS], F32)
 
-        def store_cell(half):
-            cols = half_cols[half]
-            nc.scalar.copy(out=cell_out[:, cols, :], in_=cells[:, :, cols].rearrange("p j n -> p n j"))
-            nc.sync.dma_start(out=out_1[:, cols, :], in_=cell_out[:, cols, :])
+        def both_layers(out, gate, other, cols, op):
+            nc.vector.tensor_tensor(
+                out=out[:, cols, :],
+                in0=values[:, gate, :, cols].rearrange("p j n -> p n j"),
+                in1=values[:, other, :, cols].rearrange("p j n -> p n j"),
+                op=op,
+            )
 
-        def store_hidden(half, pieces=1):
-            width = BANK // pieces
-            for start in range(BANK * half, BANK * (half + 1), width):
-                cols = slice(start, start + width)
-                nc.vector.tensor_tensor(
-                    out=hidden_out[:, cols, :],
-                    in0=values[:, GATE_O, :, cols].rearrange("p j n -> p n j"),
-                    in1=values[:, GATE_G, :, cols].rearrange("p j n -> p n j"),
-                    op=ALU.mult,
-                )
-                nc.sync.dma_start(out=out_0[:, cols, :], in_=hidden_out[:, cols, :])
+        quarter_cols = [slice(H // 4 * quarter, H // 4 * (quarter + 1)) for quarter in range(4)]
 
         engines = {mybir.EngineType.PE, mybir.EngineType.DVE, mybir.EngineType.Activation}
         with tc.manual_schedule(engines=engines):
+            add_source("ih", (GATE_F, GATE_I))
             for half, cols in enumerate(half_cols):
-                close_gate(GATE_F, half)
                 finish_gate(1, GATE_F, half)
                 times(nc.gpsimd, GATE_F, c0_sb[:, cols, 1], 1, half)
             for half in range(HALVES):
-                close_gate(GATE_I, half)
                 finish_gate(1, GATE_I, half)
-            close_gate(GATE_G, 0)
-            finish_gate(1, GATE_G, 0)
-            new_cell(1, 0)
-            close_gate(GATE_O, 0)
-            finish_gate(1, GATE_O, 0)
-            close_gate(GATE_G, 1)
-            finish_gate(1, GATE_G, 1)
-            store_hidden(0)
-            store_cell(0)
+            for half in range(HALVES):
+                close_half(GATE_G, half)
+                finish_gate(1, GATE_G, half)
+            add_source("hh", (GATE_O,))
+            first, second = half_cols
+            times(nc.vector, GATE_I, values[:, GATE_G, 1, first], 1, 0)
+            both_layers(cell_out, GATE_F, GATE_I, first, ALU.add)
+            nc.sync.dma_start(out=out_1[:, first, :], in_=cell_out[:, first, :])
+            nc.scalar.activation(out=values[:, GATE_G, 1, first], in_=cell_out[:, first, 1], func=ACT.Tanh)
             new_cell(1, 1)
-            close_gate(GATE_O, 1)
-            finish_gate(1, GATE_O, 1, pieces=2)
-            store_hidden(1, pieces=2)
-            store_cell(1)
+            nc.gpsimd.tensor_scalar(
+                out=cell_out[:, second, :],
+                in0=cells[:, :, second].rearrange("p j n -> p n j"),
+                scalar1=1.0,
+                scalar2=0.0,
+                op0=ALU.mult,
+                op1=ALU.add,
+            )
+            nc.sync.dma_start(out=out_1[:, second, :], in_=cell_out[:, second, :])
+            for half in range(HALVES):
+                close_half(GATE_O, half)
+                finish_gate(1, GATE_O, half)
+            for cols in quarter_cols:
+                both_layers(hidden_out, GATE_O, GATE_G, cols, ALU.mult)
+                nc.sync.dma_start(out=out_0[:, cols, :], in_=hidden_out[:, cols, :])

@@ -27,7 +27,6 @@ GATE_I, GATE_F, GATE_G, GATE_O = 0, 1, 2, 3
 GATES = 4
 GATE_FUNC = {GATE_I: ACT.Sigmoid, GATE_F: ACT.Sigmoid, GATE_G: ACT.Tanh, GATE_O: ACT.Sigmoid}
 PAIR = (GATE_I, GATE_F)
-SECOND_PAIR = (GATE_G, GATE_O)
 
 assert BANK == K_PASS
 
@@ -105,15 +104,16 @@ def tile_multilayerlstmcell_pb_e_kernel(
             for kpass in range(PASSES):
                 load_group(source, kpass, PAIR)
         nc.sync.dma_start(out=c0_sb[:], in_=c0)
-        for source in ("ih", "hh"):
-            for kpass in range(PASSES):
-                load_group(source, kpass, SECOND_PAIR)
+        for gate in (GATE_G, GATE_O):
+            for source in ("ih", "hh"):
+                load_gate(source, 0, gate, (slice(0, H),))
         for kpass in range(PASSES):
             load_group("hh", PASSES + kpass, PAIR)
-        load_gate("hh", 1, GATE_G, (slice(0, H),))
-        for kpass in range(PASSES):
-            load_group("ih", PASSES + kpass, PAIR)
-        load_gate("ih", 1, GATE_G, half_cols)
+        for gate in (GATE_F, GATE_I):
+            load_gate("ih", 1, gate, (slice(0, H),))
+        for cols in half_cols:
+            load_gate("hh", 1, GATE_G, (cols,))
+            load_gate("ih", 1, GATE_G, (cols,))
         load_gate("hh", 1, GATE_O, (slice(0, H),))
         load_gate("ih", 1, GATE_O, half_cols)
 
@@ -140,17 +140,16 @@ def tile_multilayerlstmcell_pb_e_kernel(
                 in_=grouped[:].rearrange("q r t -> q (r t)"),
             )
 
-        def quantise_input(kpass):
-            words = x_sb[:].bitcast(F32)
+        def turn_words(words):
             flipped = banks.tile([P, 2, P], F32, tag="bank")
-            first = kpass * K_PASS // 2
             for u in range(2):
-                nc.tensor.transpose(flipped[:, u, :], words[:, first + u : first + K_PASS // 2 : 2], ident_f32[:])
+                nc.tensor.transpose(flipped[:, u, :], words[:, u : K_PASS // 2 : 2], ident_f32[:])
             grouped = work.tile([P, P, PACK], BF16, align_bytes=64)
-            nc.vector.tensor_copy(
-                out=grouped[:].bitcast(F32), in_=flipped[:].rearrange("q u r -> q r u")
-            )
-            quantise(grouped, ("ih", 0), kpass)
+            nc.vector.tensor_copy(out=grouped[:].bitcast(F32), in_=flipped[:].rearrange("q u r -> q r u"))
+            return grouped
+
+        def quantise_input(kpass):
+            quantise(turn_words(x_sb[:, K_PASS * kpass : K_PASS * (kpass + 1)].bitcast(F32)), ("ih", 0), kpass)
 
         def quantise_states(kpass):
             words = h0_sb[:].rearrange("r k j -> r (k j)").bitcast(F32)
@@ -166,19 +165,12 @@ def tile_multilayerlstmcell_pb_e_kernel(
                 quantise(grouped, ("hh", layer), kpass)
 
         def quantise_hidden(half):
-            sorted_k = work.tile([P, PACK, P], BF16)
+            hidden = work.tile([P, BANK], BF16)
             cols = half_cols[half]
             nc.vector.tensor_tensor(
-                out=sorted_k[:],
-                in0=values[:, GATE_O, 0, cols].rearrange("r (q t) -> r t q", t=PACK),
-                in1=values[:, GATE_G, 0, cols].rearrange("r (q t) -> r t q", t=PACK),
-                op=ALU.mult,
+                out=hidden[:], in0=values[:, GATE_O, 0, cols], in1=values[:, GATE_G, 0, cols], op=ALU.mult
             )
-            flipped = banks.tile([P, PACK, P], BF16, tag="bank")
-            for t in range(PACK):
-                nc.tensor.transpose(flipped[:, t, :], sorted_k[:, t, :], ident[:])
-            grouped = work.tile([P, P, PACK], BF16, align_bytes=64)
-            nc.vector.tensor_copy(out=grouped[:], in_=flipped[:].rearrange("q t r -> q r t"))
+            grouped = turn_words(hidden[:].bitcast(F32))
             quantise(grouped, ("ih", 1), half)
 
         pick = keep.tile([P, blocks], BF16)
@@ -263,12 +255,14 @@ def tile_multilayerlstmcell_pb_e_kernel(
             times(nc.gpsimd, GATE_F, c0_sb[:, cols, 0], 0, half)
         for half in range(HALVES):
             finish_gate(0, GATE_I, half)
-        lower_sums(SECOND_PAIR)
+        lower_sums((GATE_G,))
         for half in range(HALVES):
             finish_gate(0, GATE_G, half)
         for half in range(HALVES):
-            finish_gate(0, GATE_O, half)
             new_cell(0, half)
+        lower_sums((GATE_O,))
+        for half in range(HALVES):
+            finish_gate(0, GATE_O, half)
 
         def upper_hh(kpass, gates_summed):
             for gate in gates_summed:
@@ -279,16 +273,10 @@ def tile_multilayerlstmcell_pb_e_kernel(
         for half in range(HALVES):
             quantise_hidden(half)
         upper_hh(1, PAIR)
-        for kpass in range(PASSES):
-            upper_hh(kpass, (GATE_G,))
 
-        def add_source(source, gates_summed):
+        def open_half(gate, half):
             for kpass in range(PASSES):
-                for gate in gates_summed:
-                    for half in range(HALVES):
-                        opens = source == "hh" and kpass == 0
-                        closes = source == "ih" and kpass == PASSES - 1
-                        add_pass(1, source, kpass, gate, half, start=opens, stop=closes)
+                add_pass(1, "hh", kpass, gate, half, start=(kpass == 0), stop=False)
 
         def close_half(gate, half):
             for kpass in range(PASSES):
@@ -309,34 +297,44 @@ def tile_multilayerlstmcell_pb_e_kernel(
 
         engines = {mybir.EngineType.PE, mybir.EngineType.DVE, mybir.EngineType.Activation}
         with tc.manual_schedule(engines=engines):
-            add_source("ih", (GATE_F, GATE_I))
             for half, cols in enumerate(half_cols):
+                close_half(GATE_F, half)
                 finish_gate(1, GATE_F, half)
                 times(nc.gpsimd, GATE_F, c0_sb[:, cols, 1], 1, half)
             for half in range(HALVES):
+                close_half(GATE_I, half)
                 finish_gate(1, GATE_I, half)
+            def sum_gate(gate, half):
+                open_half(gate, half)
+                close_half(gate, half)
+
+            def store_cell(quarter):
+                cols = quarter_cols[quarter]
+                both_layers(cell_out, GATE_F, GATE_I, cols, ALU.add)
+                nc.sync.dma_start(out=out_1[:, cols, :], in_=cell_out[:, cols, :])
+
+            def tanh_cell(half):
+                cols = half_cols[half]
+                nc.scalar.activation(out=values[:, GATE_G, 1, cols], in_=cell_out[:, cols, 1], func=ACT.Tanh)
+
+            sum_gate(GATE_G, 0)
+            finish_gate(1, GATE_G, 0)
+            times(nc.vector, GATE_I, values[:, GATE_G, 1, half_cols[0]], 1, 0)
+            store_cell(0)
+            sum_gate(GATE_G, 1)
+            finish_gate(1, GATE_G, 1)
+            store_cell(1)
+            tanh_cell(0)
+            times(nc.vector, GATE_I, values[:, GATE_G, 1, half_cols[1]], 1, 1)
+            store_cell(2)
             for half in range(HALVES):
-                close_half(GATE_G, half)
-                finish_gate(1, GATE_G, half)
-            add_source("hh", (GATE_O,))
-            first, second = half_cols
-            times(nc.vector, GATE_I, values[:, GATE_G, 1, first], 1, 0)
-            both_layers(cell_out, GATE_F, GATE_I, first, ALU.add)
-            nc.sync.dma_start(out=out_1[:, first, :], in_=cell_out[:, first, :])
-            nc.scalar.activation(out=values[:, GATE_G, 1, first], in_=cell_out[:, first, 1], func=ACT.Tanh)
-            new_cell(1, 1)
-            nc.gpsimd.tensor_scalar(
-                out=cell_out[:, second, :],
-                in0=cells[:, :, second].rearrange("p j n -> p n j"),
-                scalar1=1.0,
-                scalar2=0.0,
-                op0=ALU.mult,
-                op1=ALU.add,
-            )
-            nc.sync.dma_start(out=out_1[:, second, :], in_=cell_out[:, second, :])
-            for half in range(HALVES):
-                close_half(GATE_O, half)
-                finish_gate(1, GATE_O, half)
+                open_half(GATE_O, half)
+            close_half(GATE_O, 0)
+            finish_gate(1, GATE_O, 0)
+            store_cell(3)
+            tanh_cell(1)
+            close_half(GATE_O, 1)
+            finish_gate(1, GATE_O, 1)
             for cols in quarter_cols:
                 both_layers(hidden_out, GATE_O, GATE_G, cols, ALU.mult)
                 nc.sync.dma_start(out=out_0[:, cols, :], in_=hidden_out[:, cols, :])

@@ -27,6 +27,7 @@ GATE_I, GATE_F, GATE_G, GATE_O = 0, 1, 2, 3
 GATES = 4
 GATE_FUNC = {GATE_I: ACT.Sigmoid, GATE_F: ACT.Sigmoid, GATE_G: ACT.Tanh, GATE_O: ACT.Sigmoid}
 PAIR = (GATE_I, GATE_F)
+SECOND_PAIR = (GATE_G, GATE_O)
 
 assert BANK == K_PASS
 
@@ -40,18 +41,20 @@ def tile_multilayerlstmcell_pb_e_kernel(
     words_in_hbm = {"ih": W_ih_words, "hh": W_hh_words}
     scales_in_hbm = {"ih": W_ih_scales, "hh": W_hh_scales}
     half_cols = [slice(BANK * half, BANK * (half + 1)) for half in range(HALVES)]
+    quarter_cols = [slice(H // 4 * quarter, H // 4 * (quarter + 1)) for quarter in range(4)]
+    last_cols = [half_cols[0], quarter_cols[2], quarter_cols[3]]
 
     with ExitStack() as stack:
         keep = stack.enter_context(tc.tile_pool(name="keep", bufs=1))
         work = stack.enter_context(tc.tile_pool(name="work", bufs=2))
         banks = stack.enter_context(tc.psum_pool(name="banks", bufs=8))
 
+        bias_rows = keep.tile([P, BANK], BF16)
+        nc.vector.memset(bias_rows[:].bitcast(I32), 0)
         w_scales = {}
         for source in ("ih", "hh"):
             w_scales[source] = keep.tile([P, GATES * H], U8, name="w_scales_" + source, align_bytes=64)
             nc.vector.memset(w_scales[source][:].bitcast(I32), 0)
-        bias_rows = keep.tile([P, BANK], BF16)
-        nc.vector.memset(bias_rows[:], 0.0)
 
         x_sb = keep.tile([P, H], BF16)
         h0_sb = keep.tile([P, H, LAYERS], BF16)
@@ -115,7 +118,7 @@ def tile_multilayerlstmcell_pb_e_kernel(
             load_gate("hh", 1, GATE_G, (cols,))
             load_gate("ih", 1, GATE_G, (cols,))
         load_gate("hh", 1, GATE_O, (slice(0, H),))
-        load_gate("ih", 1, GATE_O, half_cols)
+        load_gate("ih", 1, GATE_O, last_cols)
 
         ident = keep.tile([P, P], BF16)
         make_identity(nc, ident[:])
@@ -204,29 +207,26 @@ def tile_multilayerlstmcell_pb_e_kernel(
 
         sums = {}
 
-        def add_pass(layer, source, kpass, gate, half, start, stop):
+        def add_pass(layer, source, kpass, gate, cols, start, stop):
             if start:
-                sums[(layer, gate, half)] = banks.tile([P, BANK], F32, name="sums_%d_%d" % (gate, half), tag="bank")
+                sums[(layer, gate, cols.start)] = banks.tile(
+                    [P, cols.stop - cols.start], F32, name="sums_%d_%d" % (gate, cols.start), tag="bank"
+                )
             group = PASSES * layer + kpass
             nc.tensor.matmul_mx(
-                out=sums[(layer, gate, half)][:],
+                out=sums[(layer, gate, cols.start)][:],
                 lhsT=a_words[(source, layer)][:, kpass, :].bitcast(FP8X4),
                 lhsT_scale=a_scales[(source, layer)][:, kpass, :],
-                rhs=w_words[(source, group, gate)][:, half_cols[half]].bitcast(FP8X4),
-                rhs_scale=w_scales[source][LIVE * group : P, H * gate + BANK * half : H * gate + BANK * (half + 1)],
+                rhs=w_words[(source, group, gate)][:, cols].bitcast(FP8X4),
+                rhs_scale=w_scales[source][LIVE * group : P, H * gate + cols.start : H * gate + cols.stop],
                 start=start,
                 stop=stop,
             )
 
-        def finish_gate(layer, gate, half, pieces=1):
-            width = BANK // pieces
-            for start in range(0, BANK, width):
-                first = BANK * half + start
-                value = values[:, gate, layer, first : first + width]
-                nc.vector.tensor_tensor(
-                    out=value, in0=sums[(layer, gate, half)][:, start : start + width], in1=value, op=ALU.add
-                )
-                nc.scalar.activation(out=value, in_=value, func=GATE_FUNC[gate])
+        def finish_gate(layer, gate, cols):
+            value = values[:, gate, layer, cols]
+            nc.vector.tensor_tensor(out=value, in0=sums[(layer, gate, cols.start)][:], in1=value, op=ALU.add)
+            nc.scalar.activation(out=value, in_=value, func=GATE_FUNC[gate])
 
         def times(engine, gate, other, layer, half):
             value = values[:, gate, layer, half_cols[half]]
@@ -246,41 +246,41 @@ def tile_multilayerlstmcell_pb_e_kernel(
         def lower_sums(gates_summed):
             for step, (source, kpass) in enumerate(steps):
                 for gate in gates_summed:
-                    for half in range(HALVES):
-                        add_pass(0, source, kpass, gate, half, start=(step == 0), stop=(step == len(steps) - 1))
+                    for cols in half_cols:
+                        add_pass(0, source, kpass, gate, cols, start=(step == 0), stop=(step == len(steps) - 1))
 
         lower_sums(PAIR)
         for half, cols in enumerate(half_cols):
-            finish_gate(0, GATE_F, half)
+            finish_gate(0, GATE_F, cols)
             times(nc.gpsimd, GATE_F, c0_sb[:, cols, 0], 0, half)
-        for half in range(HALVES):
-            finish_gate(0, GATE_I, half)
+        for cols in half_cols:
+            finish_gate(0, GATE_I, cols)
         lower_sums((GATE_G,))
-        for half in range(HALVES):
-            finish_gate(0, GATE_G, half)
+        for cols in half_cols:
+            finish_gate(0, GATE_G, cols)
         for half in range(HALVES):
             new_cell(0, half)
         lower_sums((GATE_O,))
-        for half in range(HALVES):
-            finish_gate(0, GATE_O, half)
+        for cols in half_cols:
+            finish_gate(0, GATE_O, cols)
 
         def upper_hh(kpass, gates_summed):
             for gate in gates_summed:
-                for half in range(HALVES):
-                    add_pass(1, "hh", kpass, gate, half, start=(kpass == 0), stop=False)
+                for cols in half_cols:
+                    add_pass(1, "hh", kpass, gate, cols, start=(kpass == 0), stop=False)
 
         upper_hh(0, PAIR)
         for half in range(HALVES):
             quantise_hidden(half)
         upper_hh(1, PAIR)
 
-        def open_half(gate, half):
+        def open_sums(gate, cols):
             for kpass in range(PASSES):
-                add_pass(1, "hh", kpass, gate, half, start=(kpass == 0), stop=False)
+                add_pass(1, "hh", kpass, gate, cols, start=(kpass == 0), stop=False)
 
-        def close_half(gate, half):
+        def close_sums(gate, cols):
             for kpass in range(PASSES):
-                add_pass(1, "ih", kpass, gate, half, start=False, stop=(kpass == PASSES - 1))
+                add_pass(1, "ih", kpass, gate, cols, start=False, stop=(kpass == PASSES - 1))
 
         cell_out = keep.tile([P, H, LAYERS], F32)
         hidden_out = keep.tile([P, H, LAYERS], F32)
@@ -293,48 +293,39 @@ def tile_multilayerlstmcell_pb_e_kernel(
                 op=op,
             )
 
-        quarter_cols = [slice(H // 4 * quarter, H // 4 * (quarter + 1)) for quarter in range(4)]
-
         engines = {mybir.EngineType.PE, mybir.EngineType.DVE, mybir.EngineType.Activation}
         with tc.manual_schedule(engines=engines):
             for half, cols in enumerate(half_cols):
-                close_half(GATE_F, half)
-                finish_gate(1, GATE_F, half)
+                close_sums(GATE_F, cols)
+                finish_gate(1, GATE_F, cols)
                 times(nc.gpsimd, GATE_F, c0_sb[:, cols, 1], 1, half)
-            for half in range(HALVES):
-                close_half(GATE_I, half)
-                finish_gate(1, GATE_I, half)
-            def sum_gate(gate, half):
-                open_half(gate, half)
-                close_half(gate, half)
+            for cols in half_cols:
+                close_sums(GATE_I, cols)
+                finish_gate(1, GATE_I, cols)
 
-            def store_cell(quarter):
-                cols = quarter_cols[quarter]
+            def sum_gate(gate, cols):
+                open_sums(gate, cols)
+                close_sums(gate, cols)
+
+            def new_cells(half):
+                cols = half_cols[half]
                 both_layers(cell_out, GATE_F, GATE_I, cols, ALU.add)
                 nc.sync.dma_start(out=out_1[:, cols, :], in_=cell_out[:, cols, :])
-
-            def tanh_cell(half):
-                cols = half_cols[half]
                 nc.scalar.activation(out=values[:, GATE_G, 1, cols], in_=cell_out[:, cols, 1], func=ACT.Tanh)
 
-            sum_gate(GATE_G, 0)
-            finish_gate(1, GATE_G, 0)
+            sum_gate(GATE_G, half_cols[0])
+            finish_gate(1, GATE_G, half_cols[0])
             times(nc.vector, GATE_I, values[:, GATE_G, 1, half_cols[0]], 1, 0)
-            store_cell(0)
-            sum_gate(GATE_G, 1)
-            finish_gate(1, GATE_G, 1)
-            store_cell(1)
-            tanh_cell(0)
+            sum_gate(GATE_G, half_cols[1])
+            finish_gate(1, GATE_G, half_cols[1])
+            new_cells(0)
             times(nc.vector, GATE_I, values[:, GATE_G, 1, half_cols[1]], 1, 1)
-            store_cell(2)
-            for half in range(HALVES):
-                open_half(GATE_O, half)
-            close_half(GATE_O, 0)
-            finish_gate(1, GATE_O, 0)
-            store_cell(3)
-            tanh_cell(1)
-            close_half(GATE_O, 1)
-            finish_gate(1, GATE_O, 1)
+            new_cells(1)
+            for cols in last_cols:
+                open_sums(GATE_O, cols)
+            for cols in last_cols:
+                close_sums(GATE_O, cols)
+                finish_gate(1, GATE_O, cols)
             for cols in quarter_cols:
                 both_layers(hidden_out, GATE_O, GATE_G, cols, ALU.mult)
                 nc.sync.dma_start(out=out_0[:, cols, :], in_=hidden_out[:, cols, :])

@@ -27,7 +27,7 @@ GATE_I, GATE_F, GATE_G, GATE_O = 0, 1, 2, 3
 GATES = 4
 GATE_FUNC = {GATE_I: ACT.Sigmoid, GATE_F: ACT.Sigmoid, GATE_G: ACT.Tanh, GATE_O: ACT.Sigmoid}
 PAIR = (GATE_I, GATE_F)
-SECOND_PAIR = (GATE_G, GATE_O)
+ALL = (GATE_I, GATE_F, GATE_G, GATE_O)
 
 assert BANK == K_PASS
 
@@ -42,7 +42,6 @@ def tile_multilayerlstmcell_pb_e_kernel(
     scales_in_hbm = {"ih": W_ih_scales, "hh": W_hh_scales}
     half_cols = [slice(BANK * half, BANK * (half + 1)) for half in range(HALVES)]
     quarter_cols = [slice(H // 4 * quarter, H // 4 * (quarter + 1)) for quarter in range(4)]
-    last_cols = [half_cols[0], quarter_cols[2], quarter_cols[3]]
 
     with ExitStack() as stack:
         keep = stack.enter_context(tc.tile_pool(name="keep", bufs=1))
@@ -103,13 +102,13 @@ def tile_multilayerlstmcell_pb_e_kernel(
         nc.sync.dma_start(out=bias_rows[blocks : 2 * blocks, :], in_=b_hh.rearrange("j (c n) -> (j c) n", n=BANK))
         load_scales((2, 3))
         load_scales((0, 1))
-        for source in ("ih", "hh"):
-            for kpass in range(PASSES):
-                load_group(source, kpass, PAIR)
+        for kpass in range(PASSES):
+            load_group("ih", kpass, ALL)
         nc.sync.dma_start(out=c0_sb[:], in_=c0)
+        for kpass in range(PASSES):
+            load_group("hh", kpass, PAIR)
         for gate in (GATE_G, GATE_O):
-            for source in ("ih", "hh"):
-                load_gate(source, 0, gate, (slice(0, H),))
+            load_gate("hh", 0, gate, (slice(0, H),))
         for kpass in range(PASSES):
             load_group("hh", PASSES + kpass, PAIR)
         for gate in (GATE_F, GATE_I):
@@ -117,8 +116,10 @@ def tile_multilayerlstmcell_pb_e_kernel(
         for cols in half_cols:
             load_gate("hh", 1, GATE_G, (cols,))
             load_gate("ih", 1, GATE_G, (cols,))
-        load_gate("hh", 1, GATE_O, (slice(0, H),))
-        load_gate("ih", 1, GATE_O, last_cols)
+        load_gate("hh", 1, GATE_O, half_cols[:1])
+        load_gate("ih", 1, GATE_O, half_cols[:1])
+        load_gate("hh", 1, GATE_O, half_cols[1:])
+        load_gate("ih", 1, GATE_O, quarter_cols[2:])
 
         ident = keep.tile([P, P], BF16)
         make_identity(nc, ident[:])
@@ -167,15 +168,6 @@ def tile_multilayerlstmcell_pb_e_kernel(
                 nc.vector.tensor_copy(out=grouped[:], in_=pairs[:, layer])
                 quantise(grouped, ("hh", layer), kpass)
 
-        def quantise_hidden(half):
-            hidden = work.tile([P, BANK], BF16)
-            cols = half_cols[half]
-            nc.vector.tensor_tensor(
-                out=hidden[:], in0=values[:, GATE_O, 0, cols], in1=values[:, GATE_G, 0, cols], op=ALU.mult
-            )
-            grouped = turn_words(hidden[:].bitcast(F32))
-            quantise(grouped, ("ih", 1), half)
-
         pick = keep.tile([P, blocks], BF16)
         nc.vector.tensor_tensor(out=pick[:], in0=ident[:, 0:blocks], in1=ident[:, blocks : 2 * blocks], op=ALU.add)
         values = keep.tile([P, GATES, LAYERS, H], F32)
@@ -207,7 +199,7 @@ def tile_multilayerlstmcell_pb_e_kernel(
 
         sums = {}
 
-        def add_pass(layer, source, kpass, gate, cols, start, stop):
+        def add_pass(layer, source, kpass, gate, cols, start=False, stop=False):
             if start:
                 sums[(layer, gate, cols.start)] = banks.tile(
                     [P, cols.stop - cols.start], F32, name="sums_%d_%d" % (gate, cols.start), tag="bank"
@@ -223,65 +215,20 @@ def tile_multilayerlstmcell_pb_e_kernel(
                 stop=stop,
             )
 
-        def finish_gate(layer, gate, cols):
+        def finish_gate(layer, gate, cols, bank_start):
             value = values[:, gate, layer, cols]
-            nc.vector.tensor_tensor(out=value, in0=sums[(layer, gate, cols.start)][:], in1=value, op=ALU.add)
+            bank = sums[(layer, gate, bank_start)]
+            nc.vector.tensor_tensor(
+                out=value, in0=bank[:, cols.start - bank_start : cols.stop - bank_start], in1=value, op=ALU.add
+            )
             nc.scalar.activation(out=value, in_=value, func=GATE_FUNC[gate])
 
-        def times(engine, gate, other, layer, half):
-            value = values[:, gate, layer, half_cols[half]]
+        def times(engine, layer, gate, cols, other):
+            value = values[:, gate, layer, cols]
             engine.tensor_tensor(out=value, in0=value, in1=other, op=ALU.mult)
 
-        cells = keep.tile([P, LAYERS, H], F32)
-
-        def new_cell(layer, half):
-            cols = half_cols[half]
-            times(nc.vector, GATE_I, values[:, GATE_G, layer, cols], layer, half)
-            nc.vector.tensor_tensor(
-                out=cells[:, layer, cols], in0=values[:, GATE_F, layer, cols], in1=values[:, GATE_I, layer, cols], op=ALU.add
-            )
-            nc.scalar.activation(out=values[:, GATE_G, layer, cols], in_=cells[:, layer, cols], func=ACT.Tanh)
-
-        steps = [(source, kpass) for source in ("ih", "hh") for kpass in range(PASSES)]
-        def lower_sums(gates_summed):
-            for step, (source, kpass) in enumerate(steps):
-                for gate in gates_summed:
-                    for cols in half_cols:
-                        add_pass(0, source, kpass, gate, cols, start=(step == 0), stop=(step == len(steps) - 1))
-
-        lower_sums(PAIR)
-        for half, cols in enumerate(half_cols):
-            finish_gate(0, GATE_F, cols)
-            times(nc.gpsimd, GATE_F, c0_sb[:, cols, 0], 0, half)
-        for cols in half_cols:
-            finish_gate(0, GATE_I, cols)
-        lower_sums((GATE_G,))
-        for cols in half_cols:
-            finish_gate(0, GATE_G, cols)
-        for half in range(HALVES):
-            new_cell(0, half)
-        lower_sums((GATE_O,))
-        for cols in half_cols:
-            finish_gate(0, GATE_O, cols)
-
-        def upper_hh(kpass, gates_summed):
-            for gate in gates_summed:
-                for cols in half_cols:
-                    add_pass(1, "hh", kpass, gate, cols, start=(kpass == 0), stop=False)
-
-        upper_hh(0, PAIR)
-        for half in range(HALVES):
-            quantise_hidden(half)
-        upper_hh(1, PAIR)
-
-        def open_sums(gate, cols):
-            for kpass in range(PASSES):
-                add_pass(1, "hh", kpass, gate, cols, start=(kpass == 0), stop=False)
-
-        def close_sums(gate, cols):
-            for kpass in range(PASSES):
-                add_pass(1, "ih", kpass, gate, cols, start=False, stop=(kpass == PASSES - 1))
-
+        cells = keep.tile([P, H], F32)
+        hidden = keep.tile([P, H], BF16)
         cell_out = keep.tile([P, H, LAYERS], F32)
         hidden_out = keep.tile([P, H, LAYERS], F32)
 
@@ -294,38 +241,121 @@ def tile_multilayerlstmcell_pb_e_kernel(
             )
 
         engines = {mybir.EngineType.PE, mybir.EngineType.DVE, mybir.EngineType.Activation}
-        with tc.manual_schedule(engines=engines):
-            for half, cols in enumerate(half_cols):
-                close_sums(GATE_F, cols)
-                finish_gate(1, GATE_F, cols)
-                times(nc.gpsimd, GATE_F, c0_sb[:, cols, 1], 1, half)
+        stack.enter_context(tc.manual_schedule(engines=engines))
+
+        for kpass in range(PASSES):
+            for gate in (GATE_F, GATE_I, GATE_G, GATE_O):
+                for cols in half_cols:
+                    add_pass(0, "ih", kpass, gate, cols, start=(kpass == 0))
+        for kpass in range(PASSES):
+            for gate in (GATE_F, GATE_I):
+                for cols in half_cols:
+                    add_pass(0, "hh", kpass, gate, cols, stop=(kpass == PASSES - 1))
+        for cols in half_cols:
+            finish_gate(0, GATE_F, cols, cols.start)
+            times(nc.gpsimd, 0, GATE_F, cols, c0_sb[:, cols, 0])
+        for cols in half_cols:
+            finish_gate(0, GATE_I, cols, cols.start)
+        for gate in (GATE_G, GATE_O):
             for cols in half_cols:
-                close_sums(GATE_I, cols)
-                finish_gate(1, GATE_I, cols)
+                for kpass in range(PASSES):
+                    add_pass(0, "hh", kpass, gate, cols, stop=(kpass == PASSES - 1))
+        for cols in half_cols:
+            finish_gate(0, GATE_G, cols, cols.start)
 
-            def sum_gate(gate, cols):
-                open_sums(gate, cols)
-                close_sums(gate, cols)
+        def lower_cell(cols):
+            nc.vector.tensor_tensor(
+                out=cells[:, cols], in0=values[:, GATE_F, 0, cols], in1=values[:, GATE_I, 0, cols], op=ALU.add
+            )
+            nc.scalar.activation(out=values[:, GATE_G, 0, cols], in_=cells[:, cols], func=ACT.Tanh)
 
-            def new_cells(half):
-                cols = half_cols[half]
-                both_layers(cell_out, GATE_F, GATE_I, cols, ALU.add)
-                nc.sync.dma_start(out=out_1[:, cols, :], in_=cell_out[:, cols, :])
-                nc.scalar.activation(out=values[:, GATE_G, 1, cols], in_=cell_out[:, cols, 1], func=ACT.Tanh)
+        first, second = half_cols
+        times(nc.vector, 0, GATE_I, first, values[:, GATE_G, 0, first])
+        lower_cell(first)
+        times(nc.vector, 0, GATE_I, second, values[:, GATE_G, 0, second])
+        finish_gate(0, GATE_O, first, first.start)
+        lower_cell(second)
+        finish_gate(0, GATE_O, second, second.start)
 
-            sum_gate(GATE_G, half_cols[0])
-            finish_gate(1, GATE_G, half_cols[0])
-            times(nc.vector, GATE_I, values[:, GATE_G, 1, half_cols[0]], 1, 0)
-            sum_gate(GATE_G, half_cols[1])
-            finish_gate(1, GATE_G, half_cols[1])
-            new_cells(0)
-            times(nc.vector, GATE_I, values[:, GATE_G, 1, half_cols[1]], 1, 1)
-            new_cells(1)
-            for cols in last_cols:
-                open_sums(GATE_O, cols)
-            for cols in last_cols:
-                close_sums(GATE_O, cols)
-                finish_gate(1, GATE_O, cols)
-            for cols in quarter_cols:
-                both_layers(hidden_out, GATE_O, GATE_G, cols, ALU.mult)
-                nc.sync.dma_start(out=out_0[:, cols, :], in_=hidden_out[:, cols, :])
+        def upper_hh(kpass):
+            for gate in (GATE_F, GATE_I):
+                for cols in half_cols:
+                    add_pass(1, "hh", kpass, gate, cols, start=(kpass == 0))
+
+        upper_hh(0)
+        for cols in half_cols:
+            nc.vector.tensor_tensor(
+                out=hidden[:, cols], in0=values[:, GATE_O, 0, cols], in1=values[:, GATE_G, 0, cols], op=ALU.mult
+            )
+        turned = [turn_words(hidden[:, cols].bitcast(F32)) for cols in half_cols]
+        for kpass in range(PASSES):
+            quantise(turned[kpass], ("ih", 1), kpass)
+        upper_hh(1)
+
+        def open_sums(gate, cols):
+            for kpass in range(PASSES):
+                add_pass(1, "hh", kpass, gate, cols, start=(kpass == 0))
+
+        def close_sums(gate, cols):
+            for kpass in range(PASSES):
+                add_pass(1, "ih", kpass, gate, cols, stop=(kpass == PASSES - 1))
+
+        for cols in half_cols:
+            close_sums(GATE_F, cols)
+            finish_gate(1, GATE_F, cols, cols.start)
+            times(nc.gpsimd, 1, GATE_F, cols, c0_sb[:, cols, 1])
+        for cols in half_cols:
+            close_sums(GATE_I, cols)
+            finish_gate(1, GATE_I, cols, cols.start)
+        for cols in half_cols:
+            open_sums(GATE_G, cols)
+            close_sums(GATE_G, cols)
+        open_sums(GATE_O, first)
+        close_sums(GATE_O, first)
+        for cols in quarter_cols[2:]:
+            open_sums(GATE_O, cols)
+        for cols in quarter_cols[2:]:
+            close_sums(GATE_O, cols)
+
+        def finish_quarter(gate, quarter, bank_start):
+            finish_gate(1, gate, quarter_cols[quarter], bank_start)
+
+        def times_g(quarter):
+            cols = quarter_cols[quarter]
+            times(nc.vector, 1, GATE_I, cols, values[:, GATE_G, 1, cols])
+
+        def store_cell(quarter):
+            cols = quarter_cols[quarter]
+            both_layers(cell_out, GATE_F, GATE_I, cols, ALU.add)
+            nc.sync.dma_start(out=out_1[:, cols, :], in_=cell_out[:, cols, :])
+
+        def tanh_cell(cols):
+            nc.scalar.activation(out=values[:, GATE_G, 1, cols], in_=cell_out[:, cols, 1], func=ACT.Tanh)
+
+        def store_hidden(quarter):
+            cols = quarter_cols[quarter]
+            both_layers(hidden_out, GATE_O, GATE_G, cols, ALU.mult)
+            nc.sync.dma_start(out=out_0[:, cols, :], in_=hidden_out[:, cols, :])
+
+        finish_quarter(GATE_G, 0, first.start)
+        finish_quarter(GATE_G, 1, first.start)
+        times_g(0)
+        times_g(1)
+        store_cell(0)
+        finish_quarter(GATE_G, 2, second.start)
+        finish_quarter(GATE_G, 3, second.start)
+        store_cell(1)
+        tanh_cell(first)
+        times_g(2)
+        times_g(3)
+        store_cell(2)
+        finish_quarter(GATE_O, 0, first.start)
+        store_cell(3)
+        finish_quarter(GATE_O, 1, first.start)
+        tanh_cell(second)
+        store_hidden(0)
+        finish_quarter(GATE_O, 2, quarter_cols[2].start)
+        store_hidden(1)
+        finish_quarter(GATE_O, 3, quarter_cols[3].start)
+        store_hidden(2)
+        store_hidden(3)

from contextlib import ExitStack

import concourse.mybir as mybir
from concourse.masks import make_identity

F32 = mybir.dt.float32
BF16 = mybir.dt.bfloat16
I32 = mybir.dt.int32
U32 = mybir.dt.uint32
U8 = mybir.dt.uint8
FP8X4 = mybir.dt.float8_e4m3fn_x4
ACT = mybir.ActivationFunctionType
ALU = mybir.AluOpType

P = 128
PACK = 4
K_PASS = P * PACK
H = 1024
LAYERS = 2
PASSES = H // K_PASS
BANK = 512
HALVES = H // BANK
QUADRANTS = 4
LIVE = 4

GATE_I, GATE_F, GATE_G, GATE_O = 0, 1, 2, 3
GATES = 4
GATE_FUNC = {GATE_I: ACT.Sigmoid, GATE_F: ACT.Sigmoid, GATE_G: ACT.Tanh, GATE_O: ACT.Sigmoid}
PAIR = (GATE_I, GATE_F)
ALL = (GATE_I, GATE_F, GATE_G, GATE_O)

assert BANK == K_PASS

FLOPS = 2 * P * (2 * H) * (GATES * H) * LAYERS


def tile_multilayerlstmcell_pb_e_kernel(
    tc, lstm_input, h0, c0, W_ih_words, W_ih_scales, W_hh_words, W_hh_scales, b_ih, b_hh, out_0, out_1
):
    nc = tc.nc
    words_in_hbm = {"ih": W_ih_words, "hh": W_hh_words}
    scales_in_hbm = {"ih": W_ih_scales, "hh": W_hh_scales}
    half_cols = [slice(BANK * half, BANK * (half + 1)) for half in range(HALVES)]
    quarter_cols = [slice(H // 4 * quarter, H // 4 * (quarter + 1)) for quarter in range(4)]

    with ExitStack() as stack:
        keep = stack.enter_context(tc.tile_pool(name="keep", bufs=1))
        work = stack.enter_context(tc.tile_pool(name="work", bufs=2))
        banks = stack.enter_context(tc.psum_pool(name="banks", bufs=8))

        bias_rows = keep.tile([P, BANK], BF16)
        nc.vector.memset(bias_rows[:].bitcast(I32), 0)
        w_scales = {}
        for source in ("ih", "hh"):
            w_scales[source] = keep.tile([P, GATES * H], U8, name="w_scales_" + source, align_bytes=64)
            nc.vector.memset(w_scales[source][:].bitcast(I32), 0)

        x_sb = keep.tile([P, H], BF16)
        h0_sb = keep.tile([P, H, LAYERS], BF16)
        c0_sb = keep.tile([P, H, LAYERS], BF16)
        w_words = {}

        def load_scales(quadrants):
            for source in ("ih", "hh"):
                for quadrant in quadrants:
                    nc.sync.dma_start(
                        out=w_scales[source][32 * quadrant : 32 * quadrant + 4 * LIVE, :].bitcast(I32),
                        in_=scales_in_hbm[source][:, LIVE * quadrant : LIVE * (quadrant + 1), :].bitcast(I32),
                    )

        def load_group(source, group, gates_loaded):
            width = H * len(gates_loaded)
            first = H * gates_loaded[0]
            chunk = keep.tile([P, width], U32, name="w_%s_%d_%d" % (source, group, gates_loaded[0]), align_bytes=64)
            row_words = words_in_hbm[source][group].rearrange("p n t -> p (n t)").bitcast(I32)
            nc.sync.dma_start(out=chunk[:].bitcast(I32), in_=row_words[:, first : first + width])
            for place, gate in enumerate(gates_loaded):
                w_words[(source, group, gate)] = chunk[:, H * place : H * (place + 1)]

        gate_tiles = {}

        def load_gate(source, layer, gate, pieces):
            first_group = PASSES * layer
            if (source, layer, gate) not in gate_tiles:
                chunk = keep.tile([P, PASSES, H], U32, name="w_%s_%d_%d" % (source, first_group, gate), align_bytes=64)
                gate_tiles[(source, layer, gate)] = chunk
                for kpass in range(PASSES):
                    w_words[(source, first_group + kpass, gate)] = chunk[:, kpass, :]
            row_words = (
                words_in_hbm[source][first_group : first_group + PASSES].rearrange("g p n t -> p g (n t)").bitcast(I32)
            )
            for cols in pieces:
                nc.sync.dma_start(
                    out=gate_tiles[(source, layer, gate)][:, :, cols].bitcast(I32),
                    in_=row_words[:, :, H * gate + cols.start : H * gate + cols.stop],
                )

        blocks = LAYERS * GATES * HALVES
        nc.sync.dma_start(out=x_sb[:], in_=lstm_input)
        nc.sync.dma_start(out=h0_sb[:], in_=h0)
        nc.sync.dma_start(out=bias_rows[0:blocks, :], in_=b_ih.rearrange("j (c n) -> (j c) n", n=BANK))
        nc.sync.dma_start(out=bias_rows[blocks : 2 * blocks, :], in_=b_hh.rearrange("j (c n) -> (j c) n", n=BANK))
        load_scales((2, 3))
        load_scales((0, 1))
        for kpass in range(PASSES):
            load_group("ih", kpass, ALL)
        nc.sync.dma_start(out=c0_sb[:], in_=c0)
        for kpass in range(PASSES):
            load_group("hh", kpass, PAIR)
        for gate in (GATE_G, GATE_O):
            load_gate("hh", 0, gate, (slice(0, H),))
        for kpass in range(PASSES):
            load_group("hh", PASSES + kpass, PAIR)
        for gate in (GATE_F, GATE_I):
            load_gate("ih", 1, gate, (slice(0, H),))
        for cols in half_cols:
            load_gate("hh", 1, GATE_G, (cols,))
            load_gate("ih", 1, GATE_G, (cols,))
        load_gate("hh", 1, GATE_O, half_cols[:1])
        load_gate("ih", 1, GATE_O, half_cols[:1])
        load_gate("hh", 1, GATE_O, half_cols[1:])
        load_gate("ih", 1, GATE_O, quarter_cols[2:])

        ident = keep.tile([P, P], BF16)
        make_identity(nc, ident[:])
        ident_f32 = keep.tile([P, P], F32)
        make_identity(nc, ident_f32[:])

        a_words = {}
        a_scales = {}
        for layer in range(LAYERS):
            for source in ("ih", "hh"):
                a_words[(source, layer)] = keep.tile(
                    [P, PASSES, P], U32, name="a_words_%s%d" % (source, layer), align_bytes=64
                )
                a_scales[(source, layer)] = keep.tile(
                    [P, PASSES, P], U8, name="a_scales_%s%d" % (source, layer), align_bytes=64
                )

        def quantise(grouped, operand, kpass):
            nc.vector.quantize_mx(
                out=a_words[operand][:, kpass, :].bitcast(FP8X4),
                scales=a_scales[operand][:, kpass, :],
                in_=grouped[:].rearrange("q r t -> q (r t)"),
            )

        def turn_words(words):
            flipped = banks.tile([P, 2, P], F32, tag="bank")
            for u in range(2):
                nc.tensor.transpose(flipped[:, u, :], words[:, u : K_PASS // 2 : 2], ident_f32[:])
            grouped = work.tile([P, P, PACK], BF16, align_bytes=64)
            nc.vector.tensor_copy(out=grouped[:].bitcast(F32), in_=flipped[:].rearrange("q u r -> q r u"))
            return grouped

        def quantise_input(kpass):
            quantise(turn_words(x_sb[:, K_PASS * kpass : K_PASS * (kpass + 1)].bitcast(F32)), ("ih", 0), kpass)

        def quantise_states(kpass):
            words = h0_sb[:].rearrange("r k j -> r (k j)").bitcast(F32)
            flipped = banks.tile([P, PACK, P], F32, tag="bank")
            for t in range(PACK):
                nc.tensor.transpose(
                    flipped[:, t, :], words[:, K_PASS * kpass + t : K_PASS * (kpass + 1) : PACK], ident_f32[:]
                )
            pairs = flipped[:].bitcast(BF16).rearrange("q t (r j) -> q j r t", j=LAYERS)
            for layer in range(LAYERS):
                grouped = work.tile([P, P, PACK], BF16, align_bytes=64)
                nc.vector.tensor_copy(out=grouped[:], in_=pairs[:, layer])
                quantise(grouped, ("hh", layer), kpass)

        pick = keep.tile([P, blocks], BF16)
        nc.vector.tensor_tensor(out=pick[:], in0=ident[:, 0:blocks], in1=ident[:, blocks : 2 * blocks], op=ALU.add)
        values = keep.tile([P, GATES, LAYERS, H], F32)

        def spread_biases(layer):
            for gate in (GATE_F, GATE_I, GATE_G, GATE_O):
                for half in range(HALVES):
                    block = (layer * GATES + gate) * HALVES + half
                    spread = banks.tile([P, BANK], F32, tag="bank")
                    nc.tensor.matmul(
                        out=spread[:],
                        lhsT=pick[:, block : block + 1].to_broadcast([P, P]),
                        rhs=bias_rows[:],
                        start=True,
                        stop=True,
                    )
                    target = values[:, gate, layer, half_cols[half]]
                    if half == 0:
                        nc.vector.tensor_copy(out=target, in_=spread[:])
                    else:
                        nc.scalar.copy(out=target, in_=spread[:])

        for kpass in range(PASSES):
            quantise_input(kpass)
        for kpass in range(PASSES):
            quantise_states(kpass)
        for layer in range(LAYERS):
            spread_biases(layer)

        sums = {}

        def add_pass(layer, source, kpass, gate, cols, start=False, stop=False):
            if start:
                sums[(layer, gate, cols.start)] = banks.tile(
                    [P, cols.stop - cols.start], F32, name="sums_%d_%d" % (gate, cols.start), tag="bank"
                )
            group = PASSES * layer + kpass
            nc.tensor.matmul_mx(
                out=sums[(layer, gate, cols.start)][:],
                lhsT=a_words[(source, layer)][:, kpass, :].bitcast(FP8X4),
                lhsT_scale=a_scales[(source, layer)][:, kpass, :],
                rhs=w_words[(source, group, gate)][:, cols].bitcast(FP8X4),
                rhs_scale=w_scales[source][LIVE * group : P, H * gate + cols.start : H * gate + cols.stop],
                start=start,
                stop=stop,
            )

        def finish_gate(layer, gate, cols, bank_start):
            value = values[:, gate, layer, cols]
            bank = sums[(layer, gate, bank_start)]
            nc.vector.tensor_tensor(
                out=value, in0=bank[:, cols.start - bank_start : cols.stop - bank_start], in1=value, op=ALU.add
            )
            nc.scalar.activation(out=value, in_=value, func=GATE_FUNC[gate])

        def times(engine, layer, gate, cols, other):
            value = values[:, gate, layer, cols]
            engine.tensor_tensor(out=value, in0=value, in1=other, op=ALU.mult)

        cells = keep.tile([P, H], F32)
        hidden = keep.tile([P, H], BF16)
        cell_out = keep.tile([P, H, LAYERS], F32)
        hidden_out = keep.tile([P, H, LAYERS], F32)

        def both_layers(out, gate, other, cols, op):
            nc.vector.tensor_tensor(
                out=out[:, cols, :],
                in0=values[:, gate, :, cols].rearrange("p j n -> p n j"),
                in1=values[:, other, :, cols].rearrange("p j n -> p n j"),
                op=op,
            )

        engines = {mybir.EngineType.PE, mybir.EngineType.DVE, mybir.EngineType.Activation}
        stack.enter_context(tc.manual_schedule(engines=engines))

        for kpass in range(PASSES):
            for gate in (GATE_F, GATE_I, GATE_G, GATE_O):
                for cols in half_cols:
                    add_pass(0, "ih", kpass, gate, cols, start=(kpass == 0))
        for kpass in range(PASSES):
            for gate in (GATE_F, GATE_I):
                for cols in half_cols:
                    add_pass(0, "hh", kpass, gate, cols, stop=(kpass == PASSES - 1))
        for cols in half_cols:
            finish_gate(0, GATE_F, cols, cols.start)
            times(nc.gpsimd, 0, GATE_F, cols, c0_sb[:, cols, 0])
        for cols in half_cols:
            finish_gate(0, GATE_I, cols, cols.start)
        for gate in (GATE_G, GATE_O):
            for cols in half_cols:
                for kpass in range(PASSES):
                    add_pass(0, "hh", kpass, gate, cols, stop=(kpass == PASSES - 1))
        for cols in half_cols:
            finish_gate(0, GATE_G, cols, cols.start)

        def lower_cell(cols):
            nc.vector.tensor_tensor(
                out=cells[:, cols], in0=values[:, GATE_F, 0, cols], in1=values[:, GATE_I, 0, cols], op=ALU.add
            )
            nc.scalar.activation(out=values[:, GATE_G, 0, cols], in_=cells[:, cols], func=ACT.Tanh)

        first, second = half_cols
        times(nc.vector, 0, GATE_I, first, values[:, GATE_G, 0, first])
        lower_cell(first)
        times(nc.vector, 0, GATE_I, second, values[:, GATE_G, 0, second])
        finish_gate(0, GATE_O, first, first.start)
        lower_cell(second)
        finish_gate(0, GATE_O, second, second.start)

        def upper_hh(kpass):
            for gate in (GATE_F, GATE_I):
                for cols in half_cols:
                    add_pass(1, "hh", kpass, gate, cols, start=(kpass == 0))

        upper_hh(0)
        for cols in half_cols:
            nc.vector.tensor_tensor(
                out=hidden[:, cols], in0=values[:, GATE_O, 0, cols], in1=values[:, GATE_G, 0, cols], op=ALU.mult
            )
        turned = [turn_words(hidden[:, cols].bitcast(F32)) for cols in half_cols]
        for kpass in range(PASSES):
            quantise(turned[kpass], ("ih", 1), kpass)
        upper_hh(1)

        def open_sums(gate, cols):
            for kpass in range(PASSES):
                add_pass(1, "hh", kpass, gate, cols, start=(kpass == 0))

        def close_sums(gate, cols):
            for kpass in range(PASSES):
                add_pass(1, "ih", kpass, gate, cols, stop=(kpass == PASSES - 1))

        for cols in half_cols:
            close_sums(GATE_F, cols)
            finish_gate(1, GATE_F, cols, cols.start)
            times(nc.gpsimd, 1, GATE_F, cols, c0_sb[:, cols, 1])
        for cols in half_cols:
            close_sums(GATE_I, cols)
            finish_gate(1, GATE_I, cols, cols.start)
        for cols in half_cols:
            open_sums(GATE_G, cols)
            close_sums(GATE_G, cols)
        open_sums(GATE_O, first)
        close_sums(GATE_O, first)
        for cols in quarter_cols[2:]:
            open_sums(GATE_O, cols)
        for cols in quarter_cols[2:]:
            close_sums(GATE_O, cols)

        def finish_quarter(gate, quarter, bank_start):
            finish_gate(1, gate, quarter_cols[quarter], bank_start)

        def times_g(quarter):
            cols = quarter_cols[quarter]
            times(nc.vector, 1, GATE_I, cols, values[:, GATE_G, 1, cols])

        def store_cell(quarter):
            cols = quarter_cols[quarter]
            both_layers(cell_out, GATE_F, GATE_I, cols, ALU.add)
            nc.sync.dma_start(out=out_1[:, cols, :], in_=cell_out[:, cols, :])

        def tanh_cell(cols):
            nc.scalar.activation(out=values[:, GATE_G, 1, cols], in_=cell_out[:, cols, 1], func=ACT.Tanh)

        def store_hidden(quarter):
            cols = quarter_cols[quarter]
            both_layers(hidden_out, GATE_O, GATE_G, cols, ALU.mult)
            nc.sync.dma_start(out=out_0[:, cols, :], in_=hidden_out[:, cols, :])

        finish_quarter(GATE_G, 0, first.start)
        finish_quarter(GATE_G, 1, first.start)
        times_g(0)
        times_g(1)
        store_cell(0)
        finish_quarter(GATE_G, 2, second.start)
        finish_quarter(GATE_G, 3, second.start)
        store_cell(1)
        tanh_cell(first)
        times_g(2)
        times_g(3)
        store_cell(2)
        finish_quarter(GATE_O, 0, first.start)
        store_cell(3)
        finish_quarter(GATE_O, 1, first.start)
        tanh_cell(second)
        store_hidden(0)
        finish_quarter(GATE_O, 2, quarter_cols[2].start)
        store_hidden(1)
        finish_quarter(GATE_O, 3, quarter_cols[3].start)
        store_hidden(2)
        store_hidden(3)
